import numpy as np
import ml_dtypes


def mxq(x, axis, fmt="e4m3"):
    dtype, down = {"e4m3": (ml_dtypes.float8_e4m3fn, 7), "e5m2": (ml_dtypes.float8_e5m2, 14)}[fmt]
    v = np.moveaxis(np.asarray(x, np.float32).astype(ml_dtypes.bfloat16).astype(np.float64), axis, -1)
    blocks = v.reshape(v.shape[:-1] + (-1, 32))
    amax = np.abs(blocks).max(-1, keepdims=True)
    byte = np.maximum(np.where(amax > 0, np.frexp(amax)[1] - 1 + 127, 0) - down, 1)
    scale = np.exp2(byte - 127.0)
    codes = (blocks / scale).astype(np.float32).astype(dtype).astype(np.float64)
    return np.moveaxis((codes * scale).reshape(v.shape), -1, axis)


WIDE = False


def mx_kscale(k):
    if not WIDE:
        return np.ones(k)
    levels = np.array([10, -10, 5, -5, 0])
    a = np.random.permutation(np.resize(levels, k // 512 * 4)).reshape(k // 512, 4)
    idx = np.arange(k)
    return np.exp2(a[idx // 512, idx % 128 // 32])


BF16 = ml_dtypes.bfloat16


def bf(x):
    return np.asarray(x, np.float32).astype(BF16)


def f64(x):
    return np.asarray(x).astype(np.float64)


N, IN, HID, OUT, MLP, NF = 2048, 256, 512, 512, 512, 8
FS = N // NF
G = 3 * HID


def sigmoid(v):
    return 1.0 / (1.0 + np.exp(-v))


def draw_hiddens():
    amp = 0.2 + 0.8 * np.random.random((N, 1))
    centre = np.repeat(np.random.standard_normal((NF, HID)), FS, axis=0)
    return amp * np.random.standard_normal((N, HID)) + 0.3 * centre


def setup_inputs():
    s = mx_kscale(OUT)
    return {
        "ag_diff": bf(np.random.standard_normal((N, OUT)) * 2.0 * s),
        "tension": bf(2.5 + 3.5 * np.random.random((N, 1))),
        "hiddens": bf(draw_hiddens()),
        "W_io": bf(np.random.standard_normal((G, OUT)) * 0.4 / np.sqrt(OUT) / s),
        "w_it": bf(np.random.standard_normal(G) * 0.1),
        "W_hh": bf(np.random.standard_normal((G, HID)) / np.sqrt(HID)),
        "b_ih": bf(np.random.standard_normal(G) * 0.1),
        "b_hh": bf(np.random.standard_normal(G) * 0.1),
    }


def reference(ag_diff, tension, hiddens, W_io, w_it, W_hh, b_ih, b_hh):
    h = f64(hiddens)
    gi = (mxq(f64(ag_diff), 1, "e4m3") @ mxq(f64(W_io), 1, "e4m3").T) + f64(tension) * f64(w_it) + f64(b_ih)
    gh = (mxq(h, 1, "e4m3") @ mxq(f64(W_hh), 1, "e4m3").T) + f64(b_hh)
    i_r, i_z, i_n = np.split(gi, 3, axis=-1)
    h_r, h_z, h_n = np.split(gh, 3, axis=-1)
    r = sigmoid(i_r + h_r)
    z = sigmoid(i_z + h_z)
    n = np.tanh(i_n + r * h_n)
    new_h = (1.0 - z) * n + z * h
    nh = new_h.reshape(NF, FS, HID)
    fmean = nh.mean(axis=1, keepdims=True)
    return (0.85 * nh + 0.15 * fmean).reshape(N, HID)

@@ -1,0 +1,388 @@
+from contextlib import ExitStack
+
+import concourse.mybir as mybir
+from concourse.masks import make_identity
+
+F32 = mybir.dt.float32
+BF16 = mybir.dt.bfloat16
+U32 = mybir.dt.uint32
+U8 = mybir.dt.uint8
+FP8X4 = mybir.dt.float8_e4m3fn_x4
+ALU = mybir.AluOpType
+ACT = mybir.ActivationFunctionType
+
+P = 128
+CELLS = 2048
+HID = 512
+FAC = 256
+FLOPS = 2 * 2 * CELLS * HID * 3 * HID
+KAPPA = 0.15 / (0.85 * FAC)
+RANGES = ((0, 512), (512, 512), (1024, 512), (1536, 512))
+MANUAL = True
+G5_ON_G = False
+G6_ON_G = True
+LA = 0
+LB = 1
+WB = 3
+
+
+def tile_phiaslossengine_pb_kernel(tc, ag_diff, tension, hiddens, W_io, w_it, W_hh, b_ih, b_hh, out):
+    nc = tc.nc
+    with ExitStack() as ctx:
+        const = ctx.enter_context(tc.tile_pool(name="const", bufs=1))
+        grp = ctx.enter_context(tc.tile_pool(name="grp", bufs=4))
+        work = ctx.enter_context(tc.tile_pool(name="work", bufs=WB))
+        small = ctx.enter_context(tc.tile_pool(name="small", bufs=4))
+        outp = ctx.enter_context(tc.tile_pool(name="outp", bufs=4))
+        psum = ctx.enter_context(tc.psum_pool(name="psum", bufs=1))
+        if MANUAL:
+            ctx.enter_context(tc.manual_schedule())
+
+        ident = const.tile([P, P], F32, name="ident")
+        identb = const.tile([P, P], BF16, name="identb")
+        vrows = [const.tile([P, P], F32, name="vrow%d" % v) for v in range(4)]
+        vec = const.tile([P, 36], F32, name="vec")
+        brz = const.tile([P, 8], F32, name="brz")
+        dum = const.tile([P, 2], F32, name="dum")
+        tb = const.tile([P, CELLS], F32, name="tb")
+        raw = {
+            "a": const.tile([P, 16, HID], BF16, name="a_raw"),
+            "h": const.tile([P, 16, HID], BF16, name="h_raw"),
+            "wio": const.tile([P, 6, 2, HID], BF16, name="wio_raw"),
+            "whh": const.tile([P, 6, 2, HID], BF16, name="whh_raw"),
+        }
+        gh = const.tile([P, 8, 2, P, 4], BF16, name="gh", align_bytes=64)
+        width = {"a": CELLS, "h": CELLS, "wio": 3 * HID, "whh": 3 * HID}
+        code = {}
+        scl = {}
+        for nm in ("a", "h", "wio", "whh"):
+            code[nm] = const.tile([P, width[nm]], U32, name="code_" + nm, align_bytes=64)
+            scl[nm] = const.tile([P, width[nm]], U8, name="scl_" + nm, align_bytes=64)
+
+        dview = {
+            "a": ag_diff.rearrange("(t p) k -> p t k", p=P),
+            "h": hiddens.rearrange("(t p) k -> p t k", p=P),
+            "wio": W_io.rearrange("(b p e) k -> p b e k", p=P, e=2),
+            "whh": W_hh.rearrange("(b p e) k -> p b e k", p=P, e=2),
+        }
+        oview = out.rearrange("(t p) j -> p t j", p=P)
+
+        units = []
+        for u in range(2):
+            for (c0, n) in RANGES:
+                for e in range(2):
+                    units.append((c0, n, u, e))
+        NU = len(units)
+
+        for v in range(4):
+            nc.vector.memset(vrows[v][:], 0.0)
+        nc.vector.memset(dum[:, 0:1], 0.0)
+        for v, src in enumerate((w_it, b_ih, b_hh)):
+            nc.sync.dma_start(out=vrows[v][0:6, :].bitcast(BF16), in_=src.rearrange("(b w) -> b w", w=2 * P))
+        nc.sync.dma_start(out=vrows[3][0:8, :].bitcast(BF16), in_=tension.rearrange("(b w) o -> b (w o)", w=2 * P))
+        nc.scalar.activation(out=dum[:, 1:2], in_=dum[:, 0:1], func=ACT.Sigmoid)
+
+        def load_act(nm, c0, n):
+            t0 = c0 // P
+            t1 = (c0 + n) // P
+            nc.sync.dma_start(out=raw[nm][:, t0:t1, :], in_=dview[nm][:, t0:t1, :])
+
+        def load_w(nm, b):
+            nc.sync.dma_start(out=raw[nm][:, b, :, :], in_=dview[nm][:, b, :, :])
+
+        banks = []
+        r0 = RANGES[0]
+        load_act("a", r0[0], r0[1])
+        load_w("wio", 0)
+        load_act("h", r0[0], r0[1])
+        load_w("whh", 0)
+        nf0 = r0[1] // FAC
+        banks.extend([("a", f) for f in range(nf0)])
+        banks.append(("wio", 0))
+        banks.extend([("h", f) for f in range(nf0)])
+        banks.append(("whh", 0))
+        for b in (2, 4):
+            load_w("wio", b)
+            load_w("whh", b)
+            banks.append(("wio", b))
+            banks.append(("whh", b))
+        for (c0, n) in RANGES[1:]:
+            load_act("a", c0, n)
+            load_act("h", c0, n)
+            for nm in ("a", "h"):
+                for f in range(c0 // FAC, (c0 + n) // FAC):
+                    banks.append((nm, f))
+        for b in (1, 3, 5):
+            load_w("wio", b)
+            load_w("whh", b)
+            banks.append(("wio", b))
+            banks.append(("whh", b))
+
+        make_identity(nc, ident[:])
+        make_identity(nc, identb[:])
+
+        st = {}
+
+        def prep_t(i, tag):
+            nm, j = banks[i]
+            xt = psum.tile([P, 2, 2, P], F32, tag=tag, name="xt%d" % i)
+            for t in range(2):
+                if nm in ("a", "h"):
+                    src = raw[nm][:, 2 * j + t, :].bitcast(F32)
+                else:
+                    src = raw[nm][:, j, t, :].bitcast(F32)
+                for w in range(2):
+                    nc.tensor.transpose(xt[:, t, w, :], src[:, w * P : (w + 1) * P], ident[:])
+            st[("xt", i)] = xt
+
+        def prep_e(i, eng):
+            nm, j = banks[i]
+            if nm == "h":
+                g = gh[:, j]
+            else:
+                gt = grp.tile([P, 2, P, 4], BF16, tag="grp", name="grp%d" % i, align_bytes=64)
+                g = gt[:]
+            src = st[("xt", i)][:].rearrange("q t w r -> q t r w")
+            if eng == "V":
+                nc.vector.tensor_copy(out=g.bitcast(F32), in_=src)
+            else:
+                nc.scalar.copy(out=g.bitcast(F32), in_=src)
+            st[("g", i)] = g
+
+        def prep_q(i):
+            nm, j = banks[i]
+            cols = slice(j * FAC, (j + 1) * FAC)
+            nc.vector.quantize_mx(
+                out=code[nm][:, cols].bitcast(FP8X4),
+                scales=scl[nm][:, cols],
+                in_=st[("g", i)].rearrange("q t r j -> q (t r j)"),
+            )
+
+        def wsl(g, u, e):
+            o = ((g * 2 + u) * 2 + e) * P
+            return slice(o, o + P)
+
+        def mx_pass(acc, nm_w, nm_x, g, k, start, stop):
+            c0, n, u, e = units[k]
+            nc.tensor.matmul_mx(
+                out=acc[:, :n],
+                lhsT=code[nm_w][:, wsl(g, u, e)].bitcast(FP8X4),
+                lhsT_scale=scl[nm_w][:, wsl(g, u, e)],
+                rhs=code[nm_x][:, c0 : c0 + n].bitcast(FP8X4),
+                rhs_scale=scl[nm_x][:, c0 : c0 + n],
+                start=start,
+                stop=stop,
+            )
+
+        def mx(k, part):
+            if part == "r" or part == "z":
+                g = 0 if part == "r" else 1
+                acc = psum.tile([P, 512], F32, tag="b%d" % g, name="p%s%d" % (part, k))
+                mx_pass(acc, "wio", "a", g, k, True, False)
+                mx_pass(acc, "whh", "h", g, k, False, True)
+                st[(part, k)] = acc
+            else:
+                acc = psum.tile([P, 512], F32, tag="b2", name="pin%d" % k)
+                mx_pass(acc, "wio", "a", 2, k, True, True)
+                st[("in", k)] = acc
+                acc = psum.tile([P, 512], F32, tag="b3", name="phn%d" % k)
+                mx_pass(acc, "whh", "h", 2, k, True, True)
+                st[("hn", k)] = acc
+
+        def vcol(v, g, k):
+            c0, n, u, e = units[k]
+            c = ((v * 3 + g) * 2 + u) * 2 + e
+            return vec[:, c : c + 1]
+
+        def tmerge(k, part, g, tag):
+            c0, n, u, e = units[k]
+            t = work.tile([P, 512], F32, tag=tag, name="%s%d" % (tag, k))
+            nc.vector.scalar_tensor_tensor(
+                out=t[:, :n], in0=tb[:, c0 : c0 + n], scalar=vcol(0, g, k), in1=st[(part, k)][:, :n], op0=ALU.mult, op1=ALU.add
+            )
+            st[(tag, k)] = t
+
+        def v1(k):
+            tmerge(k, "r", 0, "rp")
+
+        def v2(k):
+            tmerge(k, "z", 1, "zp")
+
+        def v4(k):
+            tmerge(k, "in", 2, "cc")
+
+        def sig(k, tag, g):
+            c0, n, u, e = units[k]
+            t = st[(tag, k)]
+            c = (g * 2 + u) * 2 + e
+            nc.scalar.activation(out=t[:, :n], in_=t[:, :n], func=ACT.Sigmoid, bias=brz[:, c : c + 1], scale=1.0)
+
+        def v3(k):
+            c0, n, u, e = units[k]
+            t = work.tile([P, 512], F32, tag="aa", name="aa%d" % k)
+            nc.vector.scalar_tensor_tensor(
+                out=t[:, :n], in0=st[("hn", k)][:, :n], scalar=vcol(2, 2, k), in1=st[("rp", k)][:, :n], op0=ALU.add, op1=ALU.mult
+            )
+            st[("aa", k)] = t
+
+        def v5(k):
+            c0, n, u, e = units[k]
+            t = st[("aa", k)]
+            eng = nc.gpsimd if G5_ON_G else nc.vector
+            eng.tensor_tensor(out=t[:, :n], in0=t[:, :n], in1=st[("cc", k)][:, :n], op=ALU.add)
+
+        def s3(k):
+            c0, n, u, e = units[k]
+            t = work.tile([P, 512], F32, tag="nn", name="nn%d" % k)
+            sn = small.tile([P, 2], F32, tag="sn", name="sn%d" % k)
+            for f in range(n // FAC):
+                cs = slice(f * FAC, (f + 1) * FAC)
+                nc.scalar.activation(
+                    out=t[:, cs], in_=st[("aa", k)][:, cs], func=ACT.Tanh, bias=vcol(1, 2, k), scale=1.0, accum_out=sn[:, f : f + 1]
+                )
+            st[("nn", k)] = t
+            st[("sn", k)] = sn
+
+        ghv = gh[:].rearrange("q f t r j -> q (f t r) j")
+
+        def g6(k):
+            c0, n, u, e = units[k]
+            t = work.tile([P, 512], F32, tag="dd", name="dd%d" % k)
+            eng = nc.gpsimd if G6_ON_G else nc.vector
+            eng.tensor_tensor(out=t[:, :n], in0=ghv[:, c0 : c0 + n, 2 * u + e], in1=st[("nn", k)][:, :n], op=ALU.subtract)
+            st[("dd", k)] = t
+
+        def v7(k):
+            c0, n, u, e = units[k]
+            t = st[("dd", k)]
+            nf = n // FAC
+            se = small.tile([P, 2], F32, tag="se", name="se%d" % k)
+            fm = small.tile([P, 2], F32, tag="fm", name="fm%d" % k)
+            for f in range(nf):
+                cs = slice(f * FAC, (f + 1) * FAC)
+                nc.vector.scalar_tensor_tensor(
+                    out=t[:, cs], in0=t[:, cs], scalar=1.0, in1=st[("zp", k)][:, cs], op0=ALU.mult, op1=ALU.mult,
+                    accum_out=se[:, f : f + 1],
+                )
+            nc.vector.tensor_tensor(out=fm[:, :nf], in0=st[("sn", k)][:, :nf], in1=se[:, :nf], op=ALU.add)
+            nc.vector.tensor_scalar_mul(out=fm[:, :nf], in0=fm[:, :nf], scalar1=KAPPA)
+            st[("fm", k)] = fm
+
+        def fin(k):
+            c0, n, u, e = units[k]
+            for q in range(n // FAC):
+                if e == 0:
+                    st[("fin", c0, u, q)] = psum.tile([P, 2, 2, P], F32, tag="b%d" % (4 + q), name="fin%d_%d" % (k, q))
+                bank = st[("fin", c0, u, q)]
+                for sl in range(2):
+                    cs = slice((2 * q + sl) * P, (2 * q + sl + 1) * P)
+                    dst = bank[:, sl, e, :]
+                    nc.tensor.matmul(out=dst, lhsT=st[("nn", k)][:, cs], rhs=ident[:], is_transpose=True, start=True, stop=False)
+                    nc.tensor.matmul(out=dst, lhsT=st[("dd", k)][:, cs], rhs=ident[:], is_transpose=True, start=False, stop=False)
+                    nc.tensor.matmul(
+                        out=dst, lhsT=st[("fm", k)][:, q : q + 1].to_broadcast([P, P]), rhs=ident[:], is_transpose=True,
+                        start=False, stop=True,
+                    )
+
+        def evac(k):
+            c0, n, u, e = units[k]
+            for q in range(n // FAC):
+                o = outp.tile([P, 2, P, 2], F32, tag="osb", name="osb%d_%d" % (k, q))
+                nc.scalar.mul(out=o[:], in_=st[("fin", c0, u, q)][:].rearrange("c s e p -> c s p e"), mul=0.85)
+                t0 = c0 // P + 2 * q
+                nc.sync.dma_start(
+                    out=oview[:, t0 : t0 + 2, u * FAC : (u + 1) * FAC], in_=o[:].rearrange("c s p e -> c s (p e)")
+                )
+
+        def vec_prep(tag):
+            vps = psum.tile([P, 512], F32, tag=tag, name="vps")
+            for v in range(3):
+                nc.tensor.transpose(vps[:, v * P : (v + 1) * P], vrows[v][:], ident[:])
+            for v in range(3):
+                nc.vector.tensor_copy(out=vec[:, 12 * v : 12 * v + 12], in_=vps[:, v * P : v * P + 6].bitcast(BF16))
+            nc.vector.tensor_tensor(out=brz[:], in0=vec[:, 12:20], in1=vec[:, 24:32], op=ALU.add)
+
+        def t_bcast(c, tag, eng):
+            tp = psum.tile([P, 512], F32, tag=tag, name="tp%d" % c)
+            for h in range(2):
+                r = 2 * c + h
+                nc.tensor.matmul(
+                    out=tp[:, h * FAC : (h + 1) * FAC], lhsT=identb[:, r : r + 1].to_broadcast([P, P]), rhs=vrows[3][:].bitcast(BF16),
+                    start=True, stop=True,
+                )
+            if eng == "V":
+                nc.vector.tensor_copy(out=tb[:, c * 512 : (c + 1) * 512], in_=tp[:])
+            else:
+                nc.scalar.copy(out=tb[:, c * 512 : (c + 1) * 512], in_=tp[:])
+
+        vec_prep("b4")
+        for c in range(4):
+            t_bcast(c, "b%d" % c, "V" if c % 2 == 0 else "S")
+
+        def tag_of(i):
+            return "b%d" % (4 + i % 4)
+
+        for i in range(6):
+            prep_t(i, tag_of(i))
+            prep_e(i, "S")
+            if i >= 1:
+                prep_q(i - 1)
+        for i in (6, 7):
+            prep_t(i, tag_of(i))
+            prep_e(i, "S")
+        prep_q(5)
+        mx(0, "r")
+        for i in (8, 9):
+            prep_t(i, tag_of(i))
+            prep_e(i, "S")
+        prep_q(6)
+        prep_q(7)
+        mx(0, "z")
+        v1(0)
+        sig(0, "rp", 0)
+        prep_q(8)
+        prep_q(9)
+        mx(0, "n")
+        for i in (10, 11, 12, 13):
+            prep_t(i, tag_of(i))
+        v2(0)
+        sig(0, "zp", 1)
+
+        T_at = {0: (14, 15, 16, 17), 1: (18, 19), 2: (20, 21), 3: (22, 23), 4: (24, 25), 5: (26, 27)}
+        E_at = {0: (10, 11, 12, 13), 1: (14, 15, 16, 17), 2: (18, 19), 3: (20, 21), 4: (22, 23), 5: (24, 25), 6: (26, 27)}
+        Q_at = {1: (10, 11, 12, 13), 2: (14, 15, 16, 17), 3: (18, 19), 4: (20, 21), 5: (22, 23), 6: (24, 25), 7: (26, 27)}
+
+        for k in range(NU + LB + 2):
+            for i in Q_at.get(k, ()):
+                prep_q(i)
+            if 0 < k < NU:
+                v1(k)
+                v2(k)
+            if k < NU:
+                v4(k)
+            if LA > 0 and 0 <= k - LA < NU:
+                s3(k - LA)
+                g6(k - LA)
+            if 0 < k < NU:
+                sig(k, "rp", 0)
+                sig(k, "zp", 1)
+            if 0 <= k - LB - 1 < NU and units[k - LB - 1][3] == 1:
+                evac(k - LB - 1)
+            for i in E_at.get(k, ()):
+                prep_e(i, "S")
+            if k < NU:
+                v3(k)
+                v5(k)
+            if LA == 0 and k < NU:
+                s3(k)
+                g6(k)
+            if 0 <= k - LB < NU:
+                v7(k - LB)
+            if k + 1 < NU:
+                mx(k + 1, "r")
+                mx(k + 1, "z")
+                mx(k + 1, "n")
+            if 0 <= k - LB < NU:
+                fin(k - LB)
+            for i in T_at.get(k, ()):
+                prep_t(i, tag_of(i) if k == 0 else "b%d" % (6 + i % 2))

@@ -20,7 +20,7 @@ KAPPA = 0.15 / (0.85 * FAC)
 RANGES = ((0, 512), (512, 512), (1024, 512), (1536, 512))
 MANUAL = True
 G5_ON_G = False
-G6_ON_G = True
+G6_ON_G = False
 LA = 0
 LB = 1
 WB = 3

@@ -20,10 +20,11 @@ KAPPA = 0.15 / (0.85 * FAC)
 RANGES = ((0, 512), (512, 512), (1024, 512), (1536, 512))
 MANUAL = True
 G5_ON_G = False
-G6_ON_G = False
+G6_ON_G = True
 LA = 0
+LG = 0
 LB = 1
-WB = 3
+WB = 4
 
 
 def tile_phiaslossengine_pb_kernel(tc, ag_diff, tension, hiddens, W_io, w_it, W_hh, b_ih, b_hh, out):
@@ -48,22 +49,22 @@ def tile_phiaslossengine_pb_kernel(tc, ag_diff, tension, hiddens, W_io, w_it, W_
         raw = {
             "a": const.tile([P, 16, HID], BF16, name="a_raw"),
             "h": const.tile([P, 16, HID], BF16, name="h_raw"),
-            "wio": const.tile([P, 6, 2, HID], BF16, name="wio_raw"),
-            "whh": const.tile([P, 6, 2, HID], BF16, name="whh_raw"),
+            "wio": const.tile([P, 2, 2, 3, HID], BF16, name="wio_raw"),
+            "whh": const.tile([P, 2, 2, 3, HID], BF16, name="whh_raw"),
         }
         gh = const.tile([P, 8, 2, P, 4], BF16, name="gh", align_bytes=64)
-        width = {"a": CELLS, "h": CELLS, "wio": 3 * HID, "whh": 3 * HID}
+        width = {"a": CELLS, "h": CELLS, "w": 6 * HID}
         code = {}
         scl = {}
-        for nm in ("a", "h", "wio", "whh"):
+        for nm in ("a", "h", "w"):
             code[nm] = const.tile([P, width[nm]], U32, name="code_" + nm, align_bytes=64)
             scl[nm] = const.tile([P, width[nm]], U8, name="scl_" + nm, align_bytes=64)
 
         dview = {
             "a": ag_diff.rearrange("(t p) k -> p t k", p=P),
             "h": hiddens.rearrange("(t p) k -> p t k", p=P),
-            "wio": W_io.rearrange("(b p e) k -> p b e k", p=P, e=2),
-            "whh": W_hh.rearrange("(b p e) k -> p b e k", p=P, e=2),
+            "wio": W_io.rearrange("(g u p e) k -> p u e g k", u=2, p=P, e=2),
+            "whh": W_hh.rearrange("(g u p e) k -> p u e g k", u=2, p=P, e=2),
         }
         oview = out.rearrange("(t p) j -> p t j", p=P)
 
@@ -87,36 +88,26 @@ def tile_phiaslossengine_pb_kernel(tc, ag_diff, tension, hiddens, W_io, w_it, W_
             t1 = (c0 + n) // P
             nc.sync.dma_start(out=raw[nm][:, t0:t1, :], in_=dview[nm][:, t0:t1, :])
 
-        def load_w(nm, b):
-            nc.sync.dma_start(out=raw[nm][:, b, :, :], in_=dview[nm][:, b, :, :])
+        def load_w(u, e):
+            for nm in ("wio", "whh"):
+                nc.sync.dma_start(out=raw[nm][:, u, e, :, :], in_=dview[nm][:, u, e, :, :])
+            for g in range(3):
+                banks.append(("w", (u * 2 + e) * 3 + g))
 
         banks = []
-        r0 = RANGES[0]
-        load_act("a", r0[0], r0[1])
-        load_w("wio", 0)
-        load_act("h", r0[0], r0[1])
-        load_w("whh", 0)
-        nf0 = r0[1] // FAC
-        banks.extend([("a", f) for f in range(nf0)])
-        banks.append(("wio", 0))
-        banks.extend([("h", f) for f in range(nf0)])
-        banks.append(("whh", 0))
-        for b in (2, 4):
-            load_w("wio", b)
-            load_w("whh", b)
-            banks.append(("wio", b))
-            banks.append(("whh", b))
-        for (c0, n) in RANGES[1:]:
-            load_act("a", c0, n)
-            load_act("h", c0, n)
+        def load_x(c0, n):
             for nm in ("a", "h"):
+                load_act(nm, c0, n)
                 for f in range(c0 // FAC, (c0 + n) // FAC):
                     banks.append((nm, f))
-        for b in (1, 3, 5):
-            load_w("wio", b)
-            load_w("whh", b)
-            banks.append(("wio", b))
-            banks.append(("whh", b))
+
+        load_x(RANGES[0][0], RANGES[0][1])
+        load_w(0, 0)
+        load_w(0, 1)
+        for (c0, n) in RANGES[1:]:
+            load_x(c0, n)
+        load_w(1, 0)
+        load_w(1, 1)
 
         make_identity(nc, ident[:])
         make_identity(nc, identb[:])
@@ -130,7 +121,7 @@ def tile_phiaslossengine_pb_kernel(tc, ag_diff, tension, hiddens, W_io, w_it, W_
                 if nm in ("a", "h"):
                     src = raw[nm][:, 2 * j + t, :].bitcast(F32)
                 else:
-                    src = raw[nm][:, j, t, :].bitcast(F32)
+                    src = raw[("wio", "whh")[t]][:, j // 6, (j // 3) % 2, j % 3, :].bitcast(F32)
                 for w in range(2):
                     nc.tensor.transpose(xt[:, t, w, :], src[:, w * P : (w + 1) * P], ident[:])
             st[("xt", i)] = xt
@@ -158,16 +149,16 @@ def tile_phiaslossengine_pb_kernel(tc, ag_diff, tension, hiddens, W_io, w_it, W_
                 in_=st[("g", i)].rearrange("q t r j -> q (t r j)"),
             )
 
-        def wsl(g, u, e):
-            o = ((g * 2 + u) * 2 + e) * P
+        def wsl(g, u, e, m):
+            o = (((u * 2 + e) * 3 + g) * 2 + m) * P
             return slice(o, o + P)
 
         def mx_pass(acc, nm_w, nm_x, g, k, start, stop):
             c0, n, u, e = units[k]
             nc.tensor.matmul_mx(
                 out=acc[:, :n],
-                lhsT=code[nm_w][:, wsl(g, u, e)].bitcast(FP8X4),
-                lhsT_scale=scl[nm_w][:, wsl(g, u, e)],
+                lhsT=code["w"][:, wsl(g, u, e, nm_w)].bitcast(FP8X4),
+                lhsT_scale=scl["w"][:, wsl(g, u, e, nm_w)],
                 rhs=code[nm_x][:, c0 : c0 + n].bitcast(FP8X4),
                 rhs_scale=scl[nm_x][:, c0 : c0 + n],
                 start=start,
@@ -178,15 +169,15 @@ def tile_phiaslossengine_pb_kernel(tc, ag_diff, tension, hiddens, W_io, w_it, W_
             if part == "r" or part == "z":
                 g = 0 if part == "r" else 1
                 acc = psum.tile([P, 512], F32, tag="b%d" % g, name="p%s%d" % (part, k))
-                mx_pass(acc, "wio", "a", g, k, True, False)
-                mx_pass(acc, "whh", "h", g, k, False, True)
+                mx_pass(acc, 0, "a", g, k, True, False)
+                mx_pass(acc, 1, "h", g, k, False, True)
                 st[(part, k)] = acc
             else:
                 acc = psum.tile([P, 512], F32, tag="b2", name="pin%d" % k)
-                mx_pass(acc, "wio", "a", 2, k, True, True)
+                mx_pass(acc, 0, "a", 2, k, True, True)
                 st[("in", k)] = acc
                 acc = psum.tile([P, 512], F32, tag="b3", name="phn%d" % k)
-                mx_pass(acc, "whh", "h", 2, k, True, True)
+                mx_pass(acc, 1, "h", 2, k, True, True)
                 st[("hn", k)] = acc
 
         def vcol(v, g, k):
@@ -248,7 +239,7 @@ def tile_phiaslossengine_pb_kernel(tc, ag_diff, tension, hiddens, W_io, w_it, W_
         def g6(k):
             c0, n, u, e = units[k]
             t = work.tile([P, 512], F32, tag="dd", name="dd%d" % k)
-            eng = nc.gpsimd if G6_ON_G else nc.vector
+            eng = nc.gpsimd if k < NU - 2 else nc.vector
             eng.tensor_tensor(out=t[:, :n], in0=ghv[:, c0 : c0 + n, 2 * u + e], in1=st[("nn", k)][:, :n], op=ALU.subtract)
             st[("dd", k)] = t
 
@@ -264,9 +255,20 @@ def tile_phiaslossengine_pb_kernel(tc, ag_diff, tension, hiddens, W_io, w_it, W_
                     out=t[:, cs], in0=t[:, cs], scalar=1.0, in1=st[("zp", k)][:, cs], op0=ALU.mult, op1=ALU.mult,
                     accum_out=se[:, f : f + 1],
                 )
-            nc.vector.tensor_tensor(out=fm[:, :nf], in0=st[("sn", k)][:, :nf], in1=se[:, :nf], op=ALU.add)
-            nc.vector.tensor_scalar_mul(out=fm[:, :nf], in0=fm[:, :nf], scalar1=KAPPA)
+            st[("se", k)] = se
             st[("fm", k)] = fm
+
+        def tiny_a(k):
+            snk = small.tile([P, 2], F32, tag="snk", name="snk%d" % k)
+            nc.scalar.mul(out=snk[:], in_=st[("sn", k)][:], mul=KAPPA)
+            st[("snk", k)] = snk
+
+        def tiny_b(k):
+            for f in range(units[k][1] // FAC):
+                nc.scalar.activation(
+                    out=st[("fm", k)][:, f : f + 1], in_=st[("se", k)][:, f : f + 1], func=ACT.Identity, scale=KAPPA,
+                    bias=st[("snk", k)][:, f : f + 1],
+                )
 
         def fin(k):
             c0, n, u, e = units[k]
@@ -315,74 +317,66 @@ def tile_phiaslossengine_pb_kernel(tc, ag_diff, tension, hiddens, W_io, w_it, W_
             else:
                 nc.scalar.copy(out=tb[:, c * 512 : (c + 1) * 512], in_=tp[:])
 
-        vec_prep("b4")
-        for c in range(4):
-            t_bcast(c, "b%d" % c, "V" if c % 2 == 0 else "S")
-
         def tag_of(i):
             return "b%d" % (4 + i % 4)
 
-        for i in range(6):
+        HEAD = 10
+        vec_prep("b4")
+        for i in range(HEAD):
+            if i % 2 == 0 and i < 8:
+                t_bcast(i // 2, "b%d" % (i // 2), "V")
             prep_t(i, tag_of(i))
-            prep_e(i, "S")
+            prep_e(i, "V" if i % 3 == 1 else "S")
             if i >= 1:
                 prep_q(i - 1)
-        for i in (6, 7):
-            prep_t(i, tag_of(i))
-            prep_e(i, "S")
-        prep_q(5)
+        prep_q(HEAD - 1)
         mx(0, "r")
-        for i in (8, 9):
-            prep_t(i, tag_of(i))
-            prep_e(i, "S")
-        prep_q(6)
-        prep_q(7)
         mx(0, "z")
-        v1(0)
-        sig(0, "rp", 0)
-        prep_q(8)
-        prep_q(9)
         mx(0, "n")
-        for i in (10, 11, 12, 13):
-            prep_t(i, tag_of(i))
-        v2(0)
-        sig(0, "zp", 1)
+        waves = [(10, 11, 12, 13), (14, 15, 16, 17), (18, 19), (20, 21), (22, 23), (24, 25), (26, 27)]
 
-        T_at = {0: (14, 15, 16, 17), 1: (18, 19), 2: (20, 21), 3: (22, 23), 4: (24, 25), 5: (26, 27)}
-        E_at = {0: (10, 11, 12, 13), 1: (14, 15, 16, 17), 2: (18, 19), 3: (20, 21), 4: (22, 23), 5: (24, 25), 6: (26, 27)}
-        Q_at = {1: (10, 11, 12, 13), 2: (14, 15, 16, 17), 3: (18, 19), 4: (20, 21), 5: (22, 23), 6: (24, 25), 7: (26, 27)}
+        def wave(w):
+            return waves[w] if 0 <= w < len(waves) else ()
 
-        for k in range(NU + LB + 2):
-            for i in Q_at.get(k, ()):
-                prep_q(i)
-            if 0 < k < NU:
+        def wave_t(w):
+            for i in wave(w):
+                prep_t(i, tag_of(i) if w < 2 else "b%d" % (6 + i % 2))
+
+        def on(k):
+            return 0 <= k < NU
+
+        wave_t(0)
+
+        for k in range(NU + 5):
+            if on(k - 2):
+                tiny_a(k - 2)
+            if on(k - 3):
+                tiny_b(k - 3)
+            if on(k):
                 v1(k)
                 v2(k)
-            if k < NU:
-                v4(k)
-            if LA > 0 and 0 <= k - LA < NU:
-                s3(k - LA)
-                g6(k - LA)
-            if 0 < k < NU:
                 sig(k, "rp", 0)
                 sig(k, "zp", 1)
-            if 0 <= k - LB - 1 < NU and units[k - LB - 1][3] == 1:
-                evac(k - LB - 1)
-            for i in E_at.get(k, ()):
+                v4(k)
+            for i in wave(k - 1):
+                prep_q(i)
+            if on(k - 4) and units[k - 4][3] == 1:
+                evac(k - 4)
+            for i in wave(k):
                 prep_e(i, "S")
-            if k < NU:
+            if on(k):
                 v3(k)
-                v5(k)
-            if LA == 0 and k < NU:
-                s3(k)
-                g6(k)
-            if 0 <= k - LB < NU:
-                v7(k - LB)
-            if k + 1 < NU:
+            if on(k - 1):
+                v5(k - 1)
+                s3(k - 1)
+            if on(k - 2):
+                v7(k - 2)
+            if on(k - 1):
+                g6(k - 1)
+            if on(k + 1):
                 mx(k + 1, "r")
                 mx(k + 1, "z")
                 mx(k + 1, "n")
-            if 0 <= k - LB < NU:
-                fin(k - LB)
-            for i in T_at.get(k, ()):
-                prep_t(i, tag_of(i) if k == 0 else "b%d" % (6 + i % 2))
+            if on(k - 3):
+                fin(k - 3)
+            wave_t(k + 1)

@@ -24,7 +24,7 @@ G6_ON_G = True
 LA = 0
 LG = 0
 LB = 1
-WB = 4
+WB = 6
 
 
 def tile_phiaslossengine_pb_kernel(tc, ag_diff, tension, hiddens, W_io, w_it, W_hh, b_ih, b_hh, out):
@@ -33,7 +33,7 @@ def tile_phiaslossengine_pb_kernel(tc, ag_diff, tension, hiddens, W_io, w_it, W_
         const = ctx.enter_context(tc.tile_pool(name="const", bufs=1))
         grp = ctx.enter_context(tc.tile_pool(name="grp", bufs=4))
         work = ctx.enter_context(tc.tile_pool(name="work", bufs=WB))
-        small = ctx.enter_context(tc.tile_pool(name="small", bufs=4))
+        small = ctx.enter_context(tc.tile_pool(name="small", bufs=6))
         outp = ctx.enter_context(tc.tile_pool(name="outp", bufs=4))
         psum = ctx.enter_context(tc.psum_pool(name="psum", bufs=1))
         if MANUAL:
@@ -45,7 +45,7 @@ def tile_phiaslossengine_pb_kernel(tc, ag_diff, tension, hiddens, W_io, w_it, W_
         vec = const.tile([P, 36], F32, name="vec")
         brz = const.tile([P, 8], F32, name="brz")
         dum = const.tile([P, 2], F32, name="dum")
-        tb = const.tile([P, CELLS], F32, name="tb")
+        tb = const.tile([P, CELLS], BF16, name="tb")
         raw = {
             "a": const.tile([P, 16, HID], BF16, name="a_raw"),
             "h": const.tile([P, 16, HID], BF16, name="h_raw"),
@@ -219,8 +219,11 @@ def tile_phiaslossengine_pb_kernel(tc, ag_diff, tension, hiddens, W_io, w_it, W_
         def v5(k):
             c0, n, u, e = units[k]
             t = st[("aa", k)]
-            eng = nc.gpsimd if G5_ON_G else nc.vector
-            eng.tensor_tensor(out=t[:, :n], in0=t[:, :n], in1=st[("cc", k)][:, :n], op=ALU.add)
+            if k < NU - 2:
+                nc.gpsimd.tensor_tensor(out=t[:, :FAC], in0=t[:, :FAC], in1=st[("cc", k)][:, :FAC], op=ALU.add)
+                nc.vector.tensor_tensor(out=t[:, FAC:n], in0=t[:, FAC:n], in1=st[("cc", k)][:, FAC:n], op=ALU.add)
+            else:
+                nc.vector.tensor_tensor(out=t[:, :n], in0=t[:, :n], in1=st[("cc", k)][:, :n], op=ALU.add)
 
         def s3(k):
             c0, n, u, e = units[k]
@@ -304,18 +307,15 @@ def tile_phiaslossengine_pb_kernel(tc, ag_diff, tension, hiddens, W_io, w_it, W_
                 nc.vector.tensor_copy(out=vec[:, 12 * v : 12 * v + 12], in_=vps[:, v * P : v * P + 6].bitcast(BF16))
             nc.vector.tensor_tensor(out=brz[:], in0=vec[:, 12:20], in1=vec[:, 24:32], op=ALU.add)
 
-        def t_bcast(c, tag, eng):
-            tp = psum.tile([P, 512], F32, tag=tag, name="tp%d" % c)
-            for h in range(2):
-                r = 2 * c + h
+        def t_bcast(half, tag):
+            tp = psum.tile([P, 1024], BF16, tag=tag, name="tp%d" % half)
+            for f in range(4):
+                r = 4 * half + f
                 nc.tensor.matmul(
-                    out=tp[:, h * FAC : (h + 1) * FAC], lhsT=identb[:, r : r + 1].to_broadcast([P, P]), rhs=vrows[3][:].bitcast(BF16),
+                    out=tp[:, f * FAC : (f + 1) * FAC], lhsT=identb[:, r : r + 1].to_broadcast([P, P]), rhs=vrows[3][:].bitcast(BF16),
                     start=True, stop=True,
                 )
-            if eng == "V":
-                nc.vector.tensor_copy(out=tb[:, c * 512 : (c + 1) * 512], in_=tp[:])
-            else:
-                nc.scalar.copy(out=tb[:, c * 512 : (c + 1) * 512], in_=tp[:])
+            nc.scalar.copy(out=tb[:, half * 1024 : (half + 1) * 1024], in_=tp[:])
 
         def tag_of(i):
             return "b%d" % (4 + i % 4)
@@ -323,8 +323,8 @@ def tile_phiaslossengine_pb_kernel(tc, ag_diff, tension, hiddens, W_io, w_it, W_
         HEAD = 10
         vec_prep("b4")
         for i in range(HEAD):
-            if i % 2 == 0 and i < 8:
-                t_bcast(i // 2, "b%d" % (i // 2), "V")
+            if i == 0 or i == 2:
+                t_bcast(i // 2, "b%d" % (i // 2))
             prep_t(i, tag_of(i))
             prep_e(i, "V" if i % 3 == 1 else "S")
             if i >= 1:
@@ -347,21 +347,19 @@ def tile_phiaslossengine_pb_kernel(tc, ag_diff, tension, hiddens, W_io, w_it, W_
 
         wave_t(0)
 
-        for k in range(NU + 5):
+        for k in range(NU + 7):
             if on(k - 2):
                 tiny_a(k - 2)
-            if on(k - 3):
-                tiny_b(k - 3)
+            if on(k - 4):
+                tiny_b(k - 4)
             if on(k):
                 v1(k)
                 v2(k)
                 sig(k, "rp", 0)
                 sig(k, "zp", 1)
                 v4(k)
-            for i in wave(k - 1):
-                prep_q(i)
-            if on(k - 4) and units[k - 4][3] == 1:
-                evac(k - 4)
+            if on(k - 5) and units[k - 5][3] == 1:
+                evac(k - 5)
             for i in wave(k):
                 prep_e(i, "S")
             if on(k):
@@ -369,14 +367,16 @@ def tile_phiaslossengine_pb_kernel(tc, ag_diff, tension, hiddens, W_io, w_it, W_
             if on(k - 1):
                 v5(k - 1)
                 s3(k - 1)
+            if on(k - 3):
+                v7(k - 3)
+            for i in wave(k - 1):
+                prep_q(i)
             if on(k - 2):
-                v7(k - 2)
-            if on(k - 1):
-                g6(k - 1)
+                g6(k - 2)
             if on(k + 1):
                 mx(k + 1, "r")
                 mx(k + 1, "z")
                 mx(k + 1, "n")
-            if on(k - 3):
-                fin(k - 3)
+            if on(k - 4):
+                fin(k - 4)
             wave_t(k + 1)

@@ -15,16 +15,12 @@ P = 128
 CELLS = 2048
 HID = 512
 FAC = 256
-FLOPS = 2 * 2 * CELLS * HID * 3 * HID
+RANGE = 512
+GATES = 3
+FLOPS = 2 * 2 * CELLS * HID * GATES * HID
 KAPPA = 0.15 / (0.85 * FAC)
-RANGES = ((0, 512), (512, 512), (1024, 512), (1536, 512))
-MANUAL = True
-G5_ON_G = False
-G6_ON_G = True
-LA = 0
-LG = 0
-LB = 1
-WB = 6
+LATE = 2
+HEAD = 10
 
 
 def tile_phiaslossengine_pb_kernel(tc, ag_diff, tension, hiddens, W_io, w_it, W_hh, b_ih, b_hh, out):
@@ -32,28 +28,27 @@ def tile_phiaslossengine_pb_kernel(tc, ag_diff, tension, hiddens, W_io, w_it, W_
     with ExitStack() as ctx:
         const = ctx.enter_context(tc.tile_pool(name="const", bufs=1))
         grp = ctx.enter_context(tc.tile_pool(name="grp", bufs=4))
-        work = ctx.enter_context(tc.tile_pool(name="work", bufs=WB))
-        small = ctx.enter_context(tc.tile_pool(name="small", bufs=6))
+        work = ctx.enter_context(tc.tile_pool(name="work", bufs=4))
+        small = ctx.enter_context(tc.tile_pool(name="small", bufs=4))
         outp = ctx.enter_context(tc.tile_pool(name="outp", bufs=4))
         psum = ctx.enter_context(tc.psum_pool(name="psum", bufs=1))
-        if MANUAL:
-            ctx.enter_context(tc.manual_schedule())
+        ctx.enter_context(tc.manual_schedule())
 
         ident = const.tile([P, P], F32, name="ident")
         identb = const.tile([P, P], BF16, name="identb")
         vrows = [const.tile([P, P], F32, name="vrow%d" % v) for v in range(4)]
         vec = const.tile([P, 36], F32, name="vec")
         brz = const.tile([P, 8], F32, name="brz")
-        dum = const.tile([P, 2], F32, name="dum")
+        warm = const.tile([P, 2], F32, name="warm")
         tb = const.tile([P, CELLS], BF16, name="tb")
         raw = {
-            "a": const.tile([P, 16, HID], BF16, name="a_raw"),
-            "h": const.tile([P, 16, HID], BF16, name="h_raw"),
-            "wio": const.tile([P, 2, 2, 3, HID], BF16, name="wio_raw"),
-            "whh": const.tile([P, 2, 2, 3, HID], BF16, name="whh_raw"),
+            "a": const.tile([P, CELLS // P, HID], BF16, name="a_raw"),
+            "h": const.tile([P, CELLS // P, HID], BF16, name="h_raw"),
+            "wio": const.tile([P, 2, 2, GATES, HID], BF16, name="wio_raw"),
+            "whh": const.tile([P, 2, 2, GATES, HID], BF16, name="whh_raw"),
         }
-        gh = const.tile([P, 8, 2, P, 4], BF16, name="gh", align_bytes=64)
-        width = {"a": CELLS, "h": CELLS, "w": 6 * HID}
+        gh = const.tile([P, CELLS // FAC, 2, P, 4], BF16, name="gh", align_bytes=64)
+        width = {"a": CELLS, "h": CELLS, "w": 2 * GATES * HID}
         code = {}
         scl = {}
         for nm in ("a", "h", "w"):
@@ -68,79 +63,70 @@ def tile_phiaslossengine_pb_kernel(tc, ag_diff, tension, hiddens, W_io, w_it, W_
         }
         oview = out.rearrange("(t p) j -> p t j", p=P)
 
-        units = []
-        for u in range(2):
-            for (c0, n) in RANGES:
-                for e in range(2):
-                    units.append((c0, n, u, e))
+        units = [(c0, u, e) for u in range(2) for c0 in range(0, CELLS, RANGE) for e in range(2)]
         NU = len(units)
 
         for v in range(4):
             nc.vector.memset(vrows[v][:], 0.0)
-        nc.vector.memset(dum[:, 0:1], 0.0)
+        nc.vector.memset(warm[:, 0:1], 0.0)
         for v, src in enumerate((w_it, b_ih, b_hh)):
             nc.sync.dma_start(out=vrows[v][0:6, :].bitcast(BF16), in_=src.rearrange("(b w) -> b w", w=2 * P))
         nc.sync.dma_start(out=vrows[3][0:8, :].bitcast(BF16), in_=tension.rearrange("(b w) o -> b (w o)", w=2 * P))
-        nc.scalar.activation(out=dum[:, 1:2], in_=dum[:, 0:1], func=ACT.Sigmoid)
-
-        def load_act(nm, c0, n):
-            t0 = c0 // P
-            t1 = (c0 + n) // P
-            nc.sync.dma_start(out=raw[nm][:, t0:t1, :], in_=dview[nm][:, t0:t1, :])
-
-        def load_w(u, e):
-            for nm in ("wio", "whh"):
-                nc.sync.dma_start(out=raw[nm][:, u, e, :, :], in_=dview[nm][:, u, e, :, :])
-            for g in range(3):
-                banks.append(("w", (u * 2 + e) * 3 + g))
+        nc.scalar.activation(out=warm[:, 1:2], in_=warm[:, 0:1], func=ACT.Sigmoid)
 
         banks = []
-        def load_x(c0, n):
-            for nm in ("a", "h"):
-                load_act(nm, c0, n)
-                for f in range(c0 // FAC, (c0 + n) // FAC):
-                    banks.append((nm, f))
 
-        load_x(RANGES[0][0], RANGES[0][1])
-        load_w(0, 0)
-        load_w(0, 1)
-        for (c0, n) in RANGES[1:]:
-            load_x(c0, n)
-        load_w(1, 0)
-        load_w(1, 1)
+        def load_cells(c0):
+            t0 = c0 // P
+            for nm in ("a", "h"):
+                nc.sync.dma_start(out=raw[nm][:, t0 : t0 + RANGE // P, :], in_=dview[nm][:, t0 : t0 + RANGE // P, :])
+                banks.extend([(nm, f) for f in range(c0 // FAC, (c0 + RANGE) // FAC)])
+
+        def load_weights(u, e):
+            for nm in ("wio", "whh"):
+                nc.sync.dma_start(out=raw[nm][:, u, e, :, :], in_=dview[nm][:, u, e, :, :])
+            banks.extend([("w", (u * 2 + e) * GATES + g) for g in range(GATES)])
+
+        load_cells(0)
+        load_weights(0, 0)
+        load_weights(0, 1)
+        for c0 in range(RANGE, CELLS, RANGE):
+            load_cells(c0)
+        load_weights(1, 0)
+        load_weights(1, 1)
 
         make_identity(nc, ident[:])
         make_identity(nc, identb[:])
 
         st = {}
 
-        def prep_t(i, tag):
+        def bank_transpose(i, tag):
             nm, j = banks[i]
             xt = psum.tile([P, 2, 2, P], F32, tag=tag, name="xt%d" % i)
             for t in range(2):
-                if nm in ("a", "h"):
-                    src = raw[nm][:, 2 * j + t, :].bitcast(F32)
+                if nm == "w":
+                    rows = raw[("wio", "whh")[t]][:, j // (2 * GATES), (j // GATES) % 2, j % GATES, :].bitcast(F32)
                 else:
-                    src = raw[("wio", "whh")[t]][:, j // 6, (j // 3) % 2, j % 3, :].bitcast(F32)
+                    rows = raw[nm][:, 2 * j + t, :].bitcast(F32)
                 for w in range(2):
-                    nc.tensor.transpose(xt[:, t, w, :], src[:, w * P : (w + 1) * P], ident[:])
+                    nc.tensor.transpose(xt[:, t, w, :], rows[:, w * P : (w + 1) * P], ident[:])
             st[("xt", i)] = xt
 
-        def prep_e(i, eng):
+        def bank_copy(i, engine):
             nm, j = banks[i]
             if nm == "h":
                 g = gh[:, j]
             else:
                 gt = grp.tile([P, 2, P, 4], BF16, tag="grp", name="grp%d" % i, align_bytes=64)
                 g = gt[:]
-            src = st[("xt", i)][:].rearrange("q t w r -> q t r w")
-            if eng == "V":
-                nc.vector.tensor_copy(out=g.bitcast(F32), in_=src)
+            words = st[("xt", i)][:].rearrange("q t w r -> q t r w")
+            if engine == "vector":
+                nc.vector.tensor_copy(out=g.bitcast(F32), in_=words)
             else:
-                nc.scalar.copy(out=g.bitcast(F32), in_=src)
+                nc.scalar.copy(out=g.bitcast(F32), in_=words)
             st[("g", i)] = g
 
-        def prep_q(i):
+        def bank_quantise(i):
             nm, j = banks[i]
             cols = slice(j * FAC, (j + 1) * FAC)
             nc.vector.quantize_mx(
@@ -149,157 +135,7 @@ def tile_phiaslossengine_pb_kernel(tc, ag_diff, tension, hiddens, W_io, w_it, W_
                 in_=st[("g", i)].rearrange("q t r j -> q (t r j)"),
             )
 
-        def wsl(g, u, e, m):
-            o = (((u * 2 + e) * 3 + g) * 2 + m) * P
-            return slice(o, o + P)
-
-        def mx_pass(acc, nm_w, nm_x, g, k, start, stop):
-            c0, n, u, e = units[k]
-            nc.tensor.matmul_mx(
-                out=acc[:, :n],
-                lhsT=code["w"][:, wsl(g, u, e, nm_w)].bitcast(FP8X4),
-                lhsT_scale=scl["w"][:, wsl(g, u, e, nm_w)],
-                rhs=code[nm_x][:, c0 : c0 + n].bitcast(FP8X4),
-                rhs_scale=scl[nm_x][:, c0 : c0 + n],
-                start=start,
-                stop=stop,
-            )
-
-        def mx(k, part):
-            if part == "r" or part == "z":
-                g = 0 if part == "r" else 1
-                acc = psum.tile([P, 512], F32, tag="b%d" % g, name="p%s%d" % (part, k))
-                mx_pass(acc, 0, "a", g, k, True, False)
-                mx_pass(acc, 1, "h", g, k, False, True)
-                st[(part, k)] = acc
-            else:
-                acc = psum.tile([P, 512], F32, tag="b2", name="pin%d" % k)
-                mx_pass(acc, 0, "a", 2, k, True, True)
-                st[("in", k)] = acc
-                acc = psum.tile([P, 512], F32, tag="b3", name="phn%d" % k)
-                mx_pass(acc, 1, "h", 2, k, True, True)
-                st[("hn", k)] = acc
-
-        def vcol(v, g, k):
-            c0, n, u, e = units[k]
-            c = ((v * 3 + g) * 2 + u) * 2 + e
-            return vec[:, c : c + 1]
-
-        def tmerge(k, part, g, tag):
-            c0, n, u, e = units[k]
-            t = work.tile([P, 512], F32, tag=tag, name="%s%d" % (tag, k))
-            nc.vector.scalar_tensor_tensor(
-                out=t[:, :n], in0=tb[:, c0 : c0 + n], scalar=vcol(0, g, k), in1=st[(part, k)][:, :n], op0=ALU.mult, op1=ALU.add
-            )
-            st[(tag, k)] = t
-
-        def v1(k):
-            tmerge(k, "r", 0, "rp")
-
-        def v2(k):
-            tmerge(k, "z", 1, "zp")
-
-        def v4(k):
-            tmerge(k, "in", 2, "cc")
-
-        def sig(k, tag, g):
-            c0, n, u, e = units[k]
-            t = st[(tag, k)]
-            c = (g * 2 + u) * 2 + e
-            nc.scalar.activation(out=t[:, :n], in_=t[:, :n], func=ACT.Sigmoid, bias=brz[:, c : c + 1], scale=1.0)
-
-        def v3(k):
-            c0, n, u, e = units[k]
-            t = work.tile([P, 512], F32, tag="aa", name="aa%d" % k)
-            nc.vector.scalar_tensor_tensor(
-                out=t[:, :n], in0=st[("hn", k)][:, :n], scalar=vcol(2, 2, k), in1=st[("rp", k)][:, :n], op0=ALU.add, op1=ALU.mult
-            )
-            st[("aa", k)] = t
-
-        def v5(k):
-            c0, n, u, e = units[k]
-            t = st[("aa", k)]
-            if k < NU - 2:
-                nc.gpsimd.tensor_tensor(out=t[:, :FAC], in0=t[:, :FAC], in1=st[("cc", k)][:, :FAC], op=ALU.add)
-                nc.vector.tensor_tensor(out=t[:, FAC:n], in0=t[:, FAC:n], in1=st[("cc", k)][:, FAC:n], op=ALU.add)
-            else:
-                nc.vector.tensor_tensor(out=t[:, :n], in0=t[:, :n], in1=st[("cc", k)][:, :n], op=ALU.add)
-
-        def s3(k):
-            c0, n, u, e = units[k]
-            t = work.tile([P, 512], F32, tag="nn", name="nn%d" % k)
-            sn = small.tile([P, 2], F32, tag="sn", name="sn%d" % k)
-            for f in range(n // FAC):
-                cs = slice(f * FAC, (f + 1) * FAC)
-                nc.scalar.activation(
-                    out=t[:, cs], in_=st[("aa", k)][:, cs], func=ACT.Tanh, bias=vcol(1, 2, k), scale=1.0, accum_out=sn[:, f : f + 1]
-                )
-            st[("nn", k)] = t
-            st[("sn", k)] = sn
-
-        ghv = gh[:].rearrange("q f t r j -> q (f t r) j")
-
-        def g6(k):
-            c0, n, u, e = units[k]
-            t = work.tile([P, 512], F32, tag="dd", name="dd%d" % k)
-            eng = nc.gpsimd if k < NU - 2 else nc.vector
-            eng.tensor_tensor(out=t[:, :n], in0=ghv[:, c0 : c0 + n, 2 * u + e], in1=st[("nn", k)][:, :n], op=ALU.subtract)
-            st[("dd", k)] = t
-
-        def v7(k):
-            c0, n, u, e = units[k]
-            t = st[("dd", k)]
-            nf = n // FAC
-            se = small.tile([P, 2], F32, tag="se", name="se%d" % k)
-            fm = small.tile([P, 2], F32, tag="fm", name="fm%d" % k)
-            for f in range(nf):
-                cs = slice(f * FAC, (f + 1) * FAC)
-                nc.vector.scalar_tensor_tensor(
-                    out=t[:, cs], in0=t[:, cs], scalar=1.0, in1=st[("zp", k)][:, cs], op0=ALU.mult, op1=ALU.mult,
-                    accum_out=se[:, f : f + 1],
-                )
-            st[("se", k)] = se
-            st[("fm", k)] = fm
-
-        def tiny_a(k):
-            snk = small.tile([P, 2], F32, tag="snk", name="snk%d" % k)
-            nc.scalar.mul(out=snk[:], in_=st[("sn", k)][:], mul=KAPPA)
-            st[("snk", k)] = snk
-
-        def tiny_b(k):
-            for f in range(units[k][1] // FAC):
-                nc.scalar.activation(
-                    out=st[("fm", k)][:, f : f + 1], in_=st[("se", k)][:, f : f + 1], func=ACT.Identity, scale=KAPPA,
-                    bias=st[("snk", k)][:, f : f + 1],
-                )
-
-        def fin(k):
-            c0, n, u, e = units[k]
-            for q in range(n // FAC):
-                if e == 0:
-                    st[("fin", c0, u, q)] = psum.tile([P, 2, 2, P], F32, tag="b%d" % (4 + q), name="fin%d_%d" % (k, q))
-                bank = st[("fin", c0, u, q)]
-                for sl in range(2):
-                    cs = slice((2 * q + sl) * P, (2 * q + sl + 1) * P)
-                    dst = bank[:, sl, e, :]
-                    nc.tensor.matmul(out=dst, lhsT=st[("nn", k)][:, cs], rhs=ident[:], is_transpose=True, start=True, stop=False)
-                    nc.tensor.matmul(out=dst, lhsT=st[("dd", k)][:, cs], rhs=ident[:], is_transpose=True, start=False, stop=False)
-                    nc.tensor.matmul(
-                        out=dst, lhsT=st[("fm", k)][:, q : q + 1].to_broadcast([P, P]), rhs=ident[:], is_transpose=True,
-                        start=False, stop=True,
-                    )
-
-        def evac(k):
-            c0, n, u, e = units[k]
-            for q in range(n // FAC):
-                o = outp.tile([P, 2, P, 2], F32, tag="osb", name="osb%d_%d" % (k, q))
-                nc.scalar.mul(out=o[:], in_=st[("fin", c0, u, q)][:].rearrange("c s e p -> c s p e"), mul=0.85)
-                t0 = c0 // P + 2 * q
-                nc.sync.dma_start(
-                    out=oview[:, t0 : t0 + 2, u * FAC : (u + 1) * FAC], in_=o[:].rearrange("c s p e -> c s (p e)")
-                )
-
-        def vec_prep(tag):
+        def spread_vectors(tag):
             vps = psum.tile([P, 512], F32, tag=tag, name="vps")
             for v in range(3):
                 nc.tensor.transpose(vps[:, v * P : (v + 1) * P], vrows[v][:], ident[:])
@@ -307,76 +143,199 @@ def tile_phiaslossengine_pb_kernel(tc, ag_diff, tension, hiddens, W_io, w_it, W_
                 nc.vector.tensor_copy(out=vec[:, 12 * v : 12 * v + 12], in_=vps[:, v * P : v * P + 6].bitcast(BF16))
             nc.vector.tensor_tensor(out=brz[:], in0=vec[:, 12:20], in1=vec[:, 24:32], op=ALU.add)
 
-        def t_bcast(half, tag):
+        def spread_tension(half, tag):
             tp = psum.tile([P, 1024], BF16, tag=tag, name="tp%d" % half)
             for f in range(4):
                 r = 4 * half + f
                 nc.tensor.matmul(
-                    out=tp[:, f * FAC : (f + 1) * FAC], lhsT=identb[:, r : r + 1].to_broadcast([P, P]), rhs=vrows[3][:].bitcast(BF16),
-                    start=True, stop=True,
+                    out=tp[:, f * FAC : (f + 1) * FAC],
+                    lhsT=identb[:, r : r + 1].to_broadcast([P, P]),
+                    rhs=vrows[3][:].bitcast(BF16),
+                    start=True,
+                    stop=True,
                 )
             nc.scalar.copy(out=tb[:, half * 1024 : (half + 1) * 1024], in_=tp[:])
 
-        def tag_of(i):
+        def vcol(v, g, k):
+            c0, u, e = units[k]
+            c = ((v * GATES + g) * 2 + u) * 2 + e
+            return vec[:, c : c + 1]
+
+        def mx_pass(acc, m, g, k, start, stop):
+            c0, u, e = units[k]
+            x = ("a", "h")[m]
+            o = (((u * 2 + e) * GATES + g) * 2 + m) * P
+            nc.tensor.matmul_mx(
+                out=acc[:],
+                lhsT=code["w"][:, o : o + P].bitcast(FP8X4),
+                lhsT_scale=scl["w"][:, o : o + P],
+                rhs=code[x][:, c0 : c0 + RANGE].bitcast(FP8X4),
+                rhs_scale=scl[x][:, c0 : c0 + RANGE],
+                start=start,
+                stop=stop,
+            )
+
+        def products(k):
+            for g, nm in enumerate(("r", "z")):
+                acc = psum.tile([P, RANGE], F32, tag="b%d" % g, name="p%s%d" % (nm, k))
+                mx_pass(acc, 0, g, k, True, False)
+                mx_pass(acc, 1, g, k, False, True)
+                st[(nm, k)] = acc
+            for m, nm in enumerate(("in", "hn")):
+                acc = psum.tile([P, RANGE], F32, tag="b%d" % (2 + m), name="p%s%d" % (nm, k))
+                mx_pass(acc, m, 2, k, True, True)
+                st[(nm, k)] = acc
+
+        def add_tension(k, g, src, dst):
+            c0, u, e = units[k]
+            t = work.tile([P, RANGE], F32, tag=dst, name="%s%d" % (dst, k))
+            nc.vector.scalar_tensor_tensor(
+                out=t[:], in0=tb[:, c0 : c0 + RANGE], scalar=vcol(0, g, k), in1=st[(src, k)][:], op0=ALU.mult, op1=ALU.add
+            )
+            st[(dst, k)] = t
+
+        def sigmoid(k, g, nm):
+            c0, u, e = units[k]
+            c = (g * 2 + u) * 2 + e
+            t = st[(nm, k)]
+            nc.scalar.activation(out=t[:], in_=t[:], func=ACT.Sigmoid, bias=brz[:, c : c + 1], scale=1.0)
+
+        def reset_times_hn(k):
+            t = work.tile([P, RANGE], F32, tag="aa", name="aa%d" % k)
+            nc.vector.scalar_tensor_tensor(
+                out=t[:], in0=st[("hn", k)][:], scalar=vcol(2, 2, k), in1=st[("rp", k)][:], op0=ALU.add, op1=ALU.mult
+            )
+            st[("aa", k)] = t
+
+        def add_in(k):
+            t = st[("aa", k)]
+            nc.vector.tensor_tensor(out=t[:], in0=t[:], in1=st[("cc", k)][:], op=ALU.add)
+
+        def candidate(k):
+            t = work.tile([P, RANGE], F32, tag="nn", name="nn%d" % k)
+            sn = small.tile([P, 2], F32, tag="sn", name="sn%d" % k)
+            for f in range(2):
+                cs = slice(f * FAC, (f + 1) * FAC)
+                nc.scalar.activation(
+                    out=t[:, cs], in_=st[("aa", k)][:, cs], func=ACT.Tanh, bias=vcol(1, 2, k), scale=1.0,
+                    accum_out=sn[:, f : f + 1],
+                )
+            st[("nn", k)] = t
+            st[("sn", k)] = sn
+
+        ghv = gh[:].rearrange("q f t r j -> q (f t r) j")
+
+        def h_minus_n(k):
+            c0, u, e = units[k]
+            t = work.tile([P, RANGE], F32, tag="dd", name="dd%d" % k)
+            engine = nc.gpsimd if k < NU - LATE else nc.vector
+            engine.tensor_tensor(out=t[:], in0=ghv[:, c0 : c0 + RANGE, 2 * u + e], in1=st[("nn", k)][:], op=ALU.subtract)
+            st[("dd", k)] = t
+
+        def times_z(k):
+            t = st[("dd", k)]
+            se = small.tile([P, 2], F32, tag="se", name="se%d" % k)
+            for f in range(2):
+                cs = slice(f * FAC, (f + 1) * FAC)
+                nc.vector.scalar_tensor_tensor(
+                    out=t[:, cs], in0=t[:, cs], scalar=1.0, in1=st[("zp", k)][:, cs], op0=ALU.mult, op1=ALU.mult,
+                    accum_out=se[:, f : f + 1],
+                )
+            st[("se", k)] = se
+
+        def scale_sum_n(k):
+            snk = small.tile([P, 2], F32, tag="snk", name="snk%d" % k)
+            nc.scalar.mul(out=snk[:], in_=st[("sn", k)][:], mul=KAPPA)
+            st[("snk", k)] = snk
+
+        def faction_term(k):
+            fm = small.tile([P, 2], F32, tag="fm", name="fm%d" % k)
+            for f in range(2):
+                nc.scalar.activation(
+                    out=fm[:, f : f + 1], in_=st[("se", k)][:, f : f + 1], func=ACT.Identity, scale=KAPPA,
+                    bias=st[("snk", k)][:, f : f + 1],
+                )
+            st[("fm", k)] = fm
+
+        def transpose_back(k):
+            c0, u, e = units[k]
+            for f in range(2):
+                if e == 0:
+                    st[("fin", c0, u, f)] = psum.tile([P, 2, 2, P], F32, tag="b%d" % (4 + f), name="fin%d_%d" % (k, f))
+                bank = st[("fin", c0, u, f)]
+                for t in range(2):
+                    cs = slice((2 * f + t) * P, (2 * f + t + 1) * P)
+                    terms = (st[("nn", k)][:, cs], st[("dd", k)][:, cs], st[("fm", k)][:, f : f + 1].to_broadcast([P, P]))
+                    for x, term in enumerate(terms):
+                        nc.tensor.matmul(
+                            out=bank[:, t, e, :], lhsT=term, rhs=ident[:], is_transpose=True, start=(x == 0), stop=(x == 2)
+                        )
+
+        def store(k):
+            c0, u, e = units[k]
+            for f in range(2):
+                o = outp.tile([P, 2, P, 2], F32, tag="osb", name="osb%d_%d" % (k, f))
+                nc.scalar.mul(out=o[:], in_=st[("fin", c0, u, f)][:].rearrange("c t e p -> c t p e"), mul=0.85)
+                t0 = c0 // P + 2 * f
+                nc.sync.dma_start(out=oview[:, t0 : t0 + 2, u * FAC : (u + 1) * FAC], in_=o[:].rearrange("c t p e -> c t (p e)"))
+
+        def ring4(i):
             return "b%d" % (4 + i % 4)
 
-        HEAD = 10
-        vec_prep("b4")
+        spread_vectors("b4")
         for i in range(HEAD):
             if i == 0 or i == 2:
-                t_bcast(i // 2, "b%d" % (i // 2))
-            prep_t(i, tag_of(i))
-            prep_e(i, "V" if i % 3 == 1 else "S")
+                spread_tension(i // 2, "b%d" % (i // 2))
+            bank_transpose(i, ring4(i))
+            bank_copy(i, "vector" if i % 3 == 1 else "scalar")
             if i >= 1:
-                prep_q(i - 1)
-        prep_q(HEAD - 1)
-        mx(0, "r")
-        mx(0, "z")
-        mx(0, "n")
-        waves = [(10, 11, 12, 13), (14, 15, 16, 17), (18, 19), (20, 21), (22, 23), (24, 25), (26, 27)]
+                bank_quantise(i - 1)
+        bank_quantise(HEAD - 1)
+        products(0)
+
+        rest = list(range(HEAD, len(banks)))
+        waves = [rest[0:4], rest[4:8]] + [rest[i : i + 2] for i in range(8, len(rest), 2)]
 
         def wave(w):
-            return waves[w] if 0 <= w < len(waves) else ()
+            return waves[w] if 0 <= w < len(waves) else []
 
-        def wave_t(w):
+        def wave_transpose(w):
             for i in wave(w):
-                prep_t(i, tag_of(i) if w < 2 else "b%d" % (6 + i % 2))
+                bank_transpose(i, ring4(i) if len(wave(w)) == 4 else "b%d" % (6 + i % 2))
 
         def on(k):
             return 0 <= k < NU
 
-        wave_t(0)
+        wave_transpose(0)
 
-        for k in range(NU + 7):
+        for k in range(NU + 5):
             if on(k - 2):
-                tiny_a(k - 2)
-            if on(k - 4):
-                tiny_b(k - 4)
-            if on(k):
-                v1(k)
-                v2(k)
-                sig(k, "rp", 0)
-                sig(k, "zp", 1)
-                v4(k)
-            if on(k - 5) and units[k - 5][3] == 1:
-                evac(k - 5)
-            for i in wave(k):
-                prep_e(i, "S")
-            if on(k):
-                v3(k)
-            if on(k - 1):
-                v5(k - 1)
-                s3(k - 1)
+                scale_sum_n(k - 2)
             if on(k - 3):
-                v7(k - 3)
+                faction_term(k - 3)
+            if on(k):
+                add_tension(k, 0, "r", "rp")
+                add_tension(k, 1, "z", "zp")
+                sigmoid(k, 0, "rp")
+                sigmoid(k, 1, "zp")
+                add_tension(k, 2, "in", "cc")
             for i in wave(k - 1):
-                prep_q(i)
+                bank_quantise(i)
+            if on(k - 1):
+                add_in(k - 1)
+                candidate(k - 1)
+            if on(k - 4) and units[k - 4][2] == 1:
+                store(k - 4)
+            for i in wave(k):
+                bank_copy(i, "scalar")
+            if on(k):
+                reset_times_hn(k)
             if on(k - 2):
-                g6(k - 2)
+                times_z(k - 2)
+            if on(k - 1):
+                h_minus_n(k - 1)
             if on(k + 1):
-                mx(k + 1, "r")
-                mx(k + 1, "z")
-                mx(k + 1, "n")
-            if on(k - 4):
-                fin(k - 4)
-            wave_t(k + 1)
+                products(k + 1)
+            if on(k - 3):
+                transpose_back(k - 3)
+            wave_transpose(k + 1)

@@ -256,6 +256,10 @@ def tile_phiaslossengine_pb_kernel(tc, ag_diff, tension, hiddens, W_io, w_it, W_
                     bias=st[("snk", k)][:, f : f + 1],
                 )
             st[("fm", k)] = fm
+            t = st[("nn", k)]
+            for f in range(2):
+                cs = slice(f * FAC, (f + 1) * FAC)
+                nc.scalar.activation(out=t[:, cs], in_=t[:, cs], func=ACT.Identity, bias=fm[:, f : f + 1], scale=1.0)
 
         def transpose_back(k):
             c0, u, e = units[k]
@@ -265,10 +269,10 @@ def tile_phiaslossengine_pb_kernel(tc, ag_diff, tension, hiddens, W_io, w_it, W_
                 bank = st[("fin", c0, u, f)]
                 for t in range(2):
                     cs = slice((2 * f + t) * P, (2 * f + t + 1) * P)
-                    terms = (st[("nn", k)][:, cs], st[("dd", k)][:, cs], st[("fm", k)][:, f : f + 1].to_broadcast([P, P]))
+                    terms = (st[("nn", k)][:, cs], st[("dd", k)][:, cs])
                     for x, term in enumerate(terms):
                         nc.tensor.matmul(
-                            out=bank[:, t, e, :], lhsT=term, rhs=ident[:], is_transpose=True, start=(x == 0), stop=(x == 2)
+                            out=bank[:, t, e, :], lhsT=term, rhs=ident[:], is_transpose=True, start=(x == 0), stop=(x == 1)
                         )
 
         def store(k):

@@ -20,7 +20,8 @@ GATES = 3
 FLOPS = 2 * 2 * CELLS * HID * GATES * HID
 KAPPA = 0.15 / (0.85 * FAC)
 LATE = 2
-HEAD = 10
+VC = (1, 4)
+HEAD = 7
 
 
 def tile_phiaslossengine_pb_kernel(tc, ag_diff, tension, hiddens, W_io, w_it, W_hh, b_ih, b_hh, out):
@@ -36,7 +37,7 @@ def tile_phiaslossengine_pb_kernel(tc, ag_diff, tension, hiddens, W_io, w_it, W_
 
         ident = const.tile([P, P], F32, name="ident")
         identb = const.tile([P, P], BF16, name="identb")
-        vrows = [const.tile([P, P], F32, name="vrow%d" % v) for v in range(4)]
+        vrows = const.tile([P, 4, P], F32, name="vrows")
         vec = const.tile([P, 36], F32, name="vec")
         brz = const.tile([P, 8], F32, name="brz")
         warm = const.tile([P, 2], F32, name="warm")
@@ -66,12 +67,8 @@ def tile_phiaslossengine_pb_kernel(tc, ag_diff, tension, hiddens, W_io, w_it, W_
         units = [(c0, u, e) for u in range(2) for c0 in range(0, CELLS, RANGE) for e in range(2)]
         NU = len(units)
 
-        for v in range(4):
-            nc.vector.memset(vrows[v][:], 0.0)
         nc.vector.memset(warm[:, 0:1], 0.0)
-        for v, src in enumerate((w_it, b_ih, b_hh)):
-            nc.sync.dma_start(out=vrows[v][0:6, :].bitcast(BF16), in_=src.rearrange("(b w) -> b w", w=2 * P))
-        nc.sync.dma_start(out=vrows[3][0:8, :].bitcast(BF16), in_=tension.rearrange("(b w) o -> b (w o)", w=2 * P))
+        nc.vector.memset(vrows[:], 0.0)
         nc.scalar.activation(out=warm[:, 1:2], in_=warm[:, 0:1], func=ACT.Sigmoid)
 
         banks = []
@@ -79,7 +76,9 @@ def tile_phiaslossengine_pb_kernel(tc, ag_diff, tension, hiddens, W_io, w_it, W_
         def load_cells(c0):
             t0 = c0 // P
             for nm in ("a", "h"):
-                nc.sync.dma_start(out=raw[nm][:, t0 : t0 + RANGE // P, :], in_=dview[nm][:, t0 : t0 + RANGE // P, :])
+                piece = FAC // P if c0 == 0 else RANGE // P
+                for t in range(t0, t0 + RANGE // P, piece):
+                    nc.sync.dma_start(out=raw[nm][:, t : t + piece, :], in_=dview[nm][:, t : t + piece, :])
                 banks.extend([(nm, f) for f in range(c0 // FAC, (c0 + RANGE) // FAC)])
 
         def load_weights(u, e):
@@ -88,6 +87,9 @@ def tile_phiaslossengine_pb_kernel(tc, ag_diff, tension, hiddens, W_io, w_it, W_
             banks.extend([("w", (u * 2 + e) * GATES + g) for g in range(GATES)])
 
         load_cells(0)
+        for v, src in enumerate((w_it, b_ih, b_hh)):
+            nc.sync.dma_start(out=vrows[0:6, v, :].bitcast(BF16), in_=src.rearrange("(b w) -> b w", w=2 * P))
+        nc.sync.dma_start(out=vrows[0:8, 3, :].bitcast(BF16), in_=tension.rearrange("(b w) o -> b (w o)", w=2 * P))
         load_weights(0, 0)
         load_weights(0, 1)
         for c0 in range(RANGE, CELLS, RANGE):
@@ -117,28 +119,34 @@ def tile_phiaslossengine_pb_kernel(tc, ag_diff, tension, hiddens, W_io, w_it, W_
             if nm == "h":
                 g = gh[:, j]
             else:
-                gt = grp.tile([P, 2, P, 4], BF16, tag="grp", name="grp%d" % i, align_bytes=64)
-                g = gt[:]
+                if i not in second:
+                    st[("grp", i)] = grp.tile([P, 2, 2, P, 4], BF16, tag="grp", name="grp%d" % i, align_bytes=64)
+                    g = st[("grp", i)][:, 0]
+                else:
+                    g = st[("grp", i - 1)][:, 1]
             words = st[("xt", i)][:].rearrange("q t w r -> q t r w")
             if engine == "vector":
                 nc.vector.tensor_copy(out=g.bitcast(F32), in_=words)
             else:
                 nc.scalar.copy(out=g.bitcast(F32), in_=words)
-            st[("g", i)] = g
 
         def bank_quantise(i):
+            if i in second:
+                return
             nm, j = banks[i]
-            cols = slice(j * FAC, (j + 1) * FAC)
+            n = 2 if i + 1 in second else 1
+            cols = slice(j * FAC, (j + n) * FAC)
+            src = gh[:, j : j + n] if nm == "h" else st[("grp", i)][:, 0:n]
             nc.vector.quantize_mx(
                 out=code[nm][:, cols].bitcast(FP8X4),
                 scales=scl[nm][:, cols],
-                in_=st[("g", i)].rearrange("q t r j -> q (t r j)"),
+                in_=src.rearrange("q b t r j -> q (b t r j)"),
             )
 
         def spread_vectors(tag):
             vps = psum.tile([P, 512], F32, tag=tag, name="vps")
             for v in range(3):
-                nc.tensor.transpose(vps[:, v * P : (v + 1) * P], vrows[v][:], ident[:])
+                nc.tensor.transpose(vps[:, v * P : (v + 1) * P], vrows[:, v, :], ident[:])
             for v in range(3):
                 nc.vector.tensor_copy(out=vec[:, 12 * v : 12 * v + 12], in_=vps[:, v * P : v * P + 6].bitcast(BF16))
             nc.vector.tensor_tensor(out=brz[:], in0=vec[:, 12:20], in1=vec[:, 24:32], op=ALU.add)
@@ -150,7 +158,7 @@ def tile_phiaslossengine_pb_kernel(tc, ag_diff, tension, hiddens, W_io, w_it, W_
                 nc.tensor.matmul(
                     out=tp[:, f * FAC : (f + 1) * FAC],
                     lhsT=identb[:, r : r + 1].to_broadcast([P, P]),
-                    rhs=vrows[3][:].bitcast(BF16),
+                    rhs=vrows[:, 3, :].bitcast(BF16),
                     start=True,
                     stop=True,
                 )
@@ -243,23 +251,12 @@ def tile_phiaslossengine_pb_kernel(tc, ag_diff, tension, hiddens, W_io, w_it, W_
                 )
             st[("se", k)] = se
 
-        def scale_sum_n(k):
-            snk = small.tile([P, 2], F32, tag="snk", name="snk%d" % k)
-            nc.scalar.mul(out=snk[:], in_=st[("sn", k)][:], mul=KAPPA)
-            st[("snk", k)] = snk
-
         def faction_term(k):
+            fs = small.tile([P, 2], F32, tag="fs", name="fs%d" % k)
             fm = small.tile([P, 2], F32, tag="fm", name="fm%d" % k)
-            for f in range(2):
-                nc.scalar.activation(
-                    out=fm[:, f : f + 1], in_=st[("se", k)][:, f : f + 1], func=ACT.Identity, scale=KAPPA,
-                    bias=st[("snk", k)][:, f : f + 1],
-                )
+            nc.gpsimd.tensor_tensor(out=fs[:], in0=st[("sn", k)][:], in1=st[("se", k)][:], op=ALU.add)
+            nc.gpsimd.tensor_scalar(out=fm[:], in0=fs[:], scalar1=KAPPA, scalar2=0.0, op0=ALU.mult, op1=ALU.add)
             st[("fm", k)] = fm
-            t = st[("nn", k)]
-            for f in range(2):
-                cs = slice(f * FAC, (f + 1) * FAC)
-                nc.scalar.activation(out=t[:, cs], in_=t[:, cs], func=ACT.Identity, bias=fm[:, f : f + 1], scale=1.0)
 
         def transpose_back(k):
             c0, u, e = units[k]
@@ -269,77 +266,91 @@ def tile_phiaslossengine_pb_kernel(tc, ag_diff, tension, hiddens, W_io, w_it, W_
                 bank = st[("fin", c0, u, f)]
                 for t in range(2):
                     cs = slice((2 * f + t) * P, (2 * f + t + 1) * P)
-                    terms = (st[("nn", k)][:, cs], st[("dd", k)][:, cs])
+                    terms = (st[("nn", k)][:, cs], st[("dd", k)][:, cs], st[("fm", k)][:, f : f + 1].to_broadcast([P, P]))
                     for x, term in enumerate(terms):
                         nc.tensor.matmul(
-                            out=bank[:, t, e, :], lhsT=term, rhs=ident[:], is_transpose=True, start=(x == 0), stop=(x == 1)
+                            out=bank[:, t, e, :], lhsT=term, rhs=ident[:], is_transpose=True, start=(x == 0), stop=(x == 2)
                         )
 
         def store(k):
             c0, u, e = units[k]
             for f in range(2):
                 o = outp.tile([P, 2, P, 2], F32, tag="osb", name="osb%d_%d" % (k, f))
-                nc.scalar.mul(out=o[:], in_=st[("fin", c0, u, f)][:].rearrange("c t e p -> c t p e"), mul=0.85)
+                src = st[("fin", c0, u, f)][:].rearrange("c t e p -> c t p e")
+                if k == NU - 1 and f == 1:
+                    nc.vector.tensor_scalar(out=o[:], in0=src, scalar1=0.85, scalar2=0.0, op0=ALU.mult, op1=ALU.add)
+                else:
+                    nc.scalar.mul(out=o[:], in_=src, mul=0.85)
                 t0 = c0 // P + 2 * f
                 nc.sync.dma_start(out=oview[:, t0 : t0 + 2, u * FAC : (u + 1) * FAC], in_=o[:].rearrange("c t p e -> c t (p e)"))
 
-        def ring4(i):
-            return "b%d" % (4 + i % 4)
-
-        spread_vectors("b4")
-        for i in range(HEAD):
-            if i == 0 or i == 2:
-                spread_tension(i // 2, "b%d" % (i // 2))
-            bank_transpose(i, ring4(i))
-            bank_copy(i, "vector" if i % 3 == 1 else "scalar")
-            if i >= 1:
-                bank_quantise(i - 1)
-        bank_quantise(HEAD - 1)
-        products(0)
-
         rest = list(range(HEAD, len(banks)))
-        waves = [rest[0:4], rest[4:8]] + [rest[i : i + 2] for i in range(8, len(rest), 2)]
+        waves = [rest[0:3], rest[3:7], rest[7:11]] + [rest[i : i + 2] for i in range(11, len(rest), 2)]
+        second = set()
+        for wv in waves:
+            second.update(wv[1::2])
 
         def wave(w):
             return waves[w] if 0 <= w < len(waves) else []
 
         def wave_transpose(w):
             for i in wave(w):
-                bank_transpose(i, ring4(i) if len(wave(w)) == 4 else "b%d" % (6 + i % 2))
+                bank_transpose(i, ring4(i) if w < 3 else "b%d" % (6 + i % 2))
 
         def on(k):
             return 0 <= k < NU
 
-        wave_transpose(0)
+        def ring8(i):
+            return "b%d" % (2 + i % 6) if i < 7 else "b%d" % (4 + i % 4)
+
+        def ring4(i):
+            return "b%d" % (4 + i % 4)
+
+        for i in range(HEAD):
+            if i == 4:
+                spread_vectors("b0")
+                spread_tension(0, "b1")
+                spread_tension(1, "b0")
+            bank_transpose(i, ring8(i))
+            bank_copy(i, "vector" if i in VC else "scalar")
+            if i >= 1:
+                bank_quantise(i - 1)
+        for i in wave(0):
+            bank_transpose(i, ring4(i))
+            bank_copy(i, "scalar")
+        bank_quantise(HEAD - 1)
+        products(0)
+        wave_transpose(1)
 
         for k in range(NU + 5):
-            if on(k - 2):
-                scale_sum_n(k - 2)
-            if on(k - 3):
-                faction_term(k - 3)
             if on(k):
                 add_tension(k, 0, "r", "rp")
                 add_tension(k, 1, "z", "zp")
                 sigmoid(k, 0, "rp")
                 sigmoid(k, 1, "zp")
                 add_tension(k, 2, "in", "cc")
-            for i in wave(k - 1):
+            for i in wave(k):
                 bank_quantise(i)
-            if on(k - 1):
+            if on(k - 1) and k < NU:
                 add_in(k - 1)
                 candidate(k - 1)
             if on(k - 4) and units[k - 4][2] == 1:
                 store(k - 4)
-            for i in wave(k):
+            for i in wave(k + 1):
                 bank_copy(i, "scalar")
             if on(k):
                 reset_times_hn(k)
             if on(k - 2):
                 times_z(k - 2)
+            if k == NU - 1:
+                add_in(k)
+                candidate(k)
             if on(k - 1):
                 h_minus_n(k - 1)
+            if on(k - 2):
+                faction_term(k - 2)
             if on(k + 1):
                 products(k + 1)
             if on(k - 3):
                 transpose_back(k - 3)
-            wave_transpose(k + 1)
+            wave_transpose(k + 2)

@@ -19,6 +19,7 @@ RANGE = 512
 GATES = 3
 FLOPS = 2 * 2 * CELLS * HID * GATES * HID
 KAPPA = 0.15 / (0.85 * FAC)
+ZS = [3 < k < 14 for k in range(16)]
 LATE = 2
 VC = (1, 4)
 HEAD = 7
@@ -242,6 +243,9 @@ def tile_phiaslossengine_pb_kernel(tc, ag_diff, tension, hiddens, W_io, w_it, W_
 
         def times_z(k):
             t = st[("dd", k)]
+            if ZS[k]:
+                nc.vector.tensor_tensor(out=t[:], in0=t[:], in1=st[("zp", k)][:], op=ALU.mult)
+                return
             se = small.tile([P, 2], F32, tag="se", name="se%d" % k)
             for f in range(2):
                 cs = slice(f * FAC, (f + 1) * FAC)
@@ -249,6 +253,13 @@ def tile_phiaslossengine_pb_kernel(tc, ag_diff, tension, hiddens, W_io, w_it, W_
                     out=t[:, cs], in0=t[:, cs], scalar=1.0, in1=st[("zp", k)][:, cs], op0=ALU.mult, op1=ALU.mult,
                     accum_out=se[:, f : f + 1],
                 )
+            st[("se", k)] = se
+
+        def sum_zd(k):
+            se = small.tile([P, 2], F32, tag="se", name="se%d" % k)
+            for f in range(2):
+                cs = slice(f * FAC, (f + 1) * FAC)
+                nc.scalar.activation(out=st[("zp", k)][:, cs], in_=st[("dd", k)][:, cs], func=ACT.Identity, bias=0.0, scale=1.0, accum_out=se[:, f : f + 1])
             st[("se", k)] = se
 
         def faction_term(k):
@@ -342,6 +353,8 @@ def tile_phiaslossengine_pb_kernel(tc, ag_diff, tension, hiddens, W_io, w_it, W_
                 reset_times_hn(k)
             if on(k - 2):
                 times_z(k - 2)
+                if ZS[k - 2]:
+                    sum_zd(k - 2)
             if k == NU - 1:
                 add_in(k)
                 candidate(k)

@@ -19,7 +19,9 @@ RANGE = 512
 GATES = 3
 FLOPS = 2 * 2 * CELLS * HID * GATES * HID
 KAPPA = 0.15 / (0.85 * FAC)
-ZS = [3 < k < 14 for k in range(16)]
+ZS = [3 < k < 13 for k in range(16)]
+FMS = 13
+VST = 13
 LATE = 2
 VC = (1, 4)
 HEAD = 7
@@ -265,15 +267,22 @@ def tile_phiaslossengine_pb_kernel(tc, ag_diff, tension, hiddens, W_io, w_it, W_
         def faction_term(k):
             fs = small.tile([P, 2], F32, tag="fs", name="fs%d" % k)
             fm = small.tile([P, 2], F32, tag="fm", name="fm%d" % k)
-            nc.gpsimd.tensor_tensor(out=fs[:], in0=st[("sn", k)][:], in1=st[("se", k)][:], op=ALU.add)
-            nc.gpsimd.tensor_scalar(out=fm[:], in0=fs[:], scalar1=KAPPA, scalar2=0.0, op0=ALU.mult, op1=ALU.add)
+            if k >= FMS:
+                nc.scalar.mul(out=fs[:], in_=st[("sn", k)][:], mul=KAPPA)
+                for f in range(2):
+                    nc.scalar.activation(
+                        out=fm[:, f : f + 1], in_=st[("se", k)][:, f : f + 1], func=ACT.Identity, scale=KAPPA, bias=fs[:, f : f + 1]
+                    )
+            for fc in [slice(0, 2)] if k < FMS else []:
+                nc.gpsimd.tensor_tensor(out=fs[:, fc], in0=st[("sn", k)][:, fc], in1=st[("se", k)][:, fc], op=ALU.add)
+                nc.gpsimd.tensor_scalar(out=fm[:, fc], in0=fs[:, fc], scalar1=KAPPA, scalar2=0.0, op0=ALU.mult, op1=ALU.add)
             st[("fm", k)] = fm
 
         def transpose_back(k):
             c0, u, e = units[k]
             for f in range(2):
                 if e == 0:
-                    st[("fin", c0, u, f)] = psum.tile([P, 2, 2, P], F32, tag="b%d" % (4 + f), name="fin%d_%d" % (k, f))
+                    st[("fin", c0, u, f)] = psum.tile([P, 2, 2, P], F32, tag="b%d" % (4 + f + 2 * (u * c0 // RANGE % 2)), name="fin%d_%d" % (k, f))
                 bank = st[("fin", c0, u, f)]
                 for t in range(2):
                     cs = slice((2 * f + t) * P, (2 * f + t + 1) * P)
@@ -283,12 +292,12 @@ def tile_phiaslossengine_pb_kernel(tc, ag_diff, tension, hiddens, W_io, w_it, W_
                             out=bank[:, t, e, :], lhsT=term, rhs=ident[:], is_transpose=True, start=(x == 0), stop=(x == 2)
                         )
 
-        def store(k):
+        def store(k, factions=(0, 1)):
             c0, u, e = units[k]
-            for f in range(2):
+            for f in factions:
                 o = outp.tile([P, 2, P, 2], F32, tag="osb", name="osb%d_%d" % (k, f))
                 src = st[("fin", c0, u, f)][:].rearrange("c t e p -> c t p e")
-                if k == NU - 1 and f == 1:
+                if k >= VST and f == 1:
                     nc.vector.tensor_scalar(out=o[:], in0=src, scalar1=0.85, scalar2=0.0, op0=ALU.mult, op1=ALU.add)
                 else:
                     nc.scalar.mul(out=o[:], in_=src, mul=0.85)
@@ -345,22 +354,27 @@ def tile_phiaslossengine_pb_kernel(tc, ag_diff, tension, hiddens, W_io, w_it, W_
             if on(k - 1) and k < NU:
                 add_in(k - 1)
                 candidate(k - 1)
-            if on(k - 4) and units[k - 4][2] == 1:
+            if k == NU + 1:
+                store(k - 4, (0,))
+                times_z(k - 2)
+                faction_term(k - 2)
+                store(k - 4, (1,))
+            elif on(k - 4) and units[k - 4][2] == 1:
                 store(k - 4)
             for i in wave(k + 1):
                 bank_copy(i, "scalar")
             if on(k):
                 reset_times_hn(k)
-            if on(k - 2):
+            if on(k - 2) and k <= NU:
                 times_z(k - 2)
-                if ZS[k - 2]:
-                    sum_zd(k - 2)
             if k == NU - 1:
                 add_in(k)
                 candidate(k)
+            if on(k - 2) and ZS[k - 2]:
+                sum_zd(k - 2)
             if on(k - 1):
                 h_minus_n(k - 1)
-            if on(k - 2):
+            if on(k - 2) and k <= NU:
                 faction_term(k - 2)
             if on(k + 1):
                 products(k + 1)

@@ -19,9 +19,14 @@ RANGE = 512
 GATES = 3
 FLOPS = 2 * 2 * CELLS * HID * GATES * HID
 KAPPA = 0.15 / (0.85 * FAC)
+T0 = 6
+G0 = 6
+G1 = 13
 ZS = [3 < k < 13 for k in range(16)]
 FMS = 13
 VST = 13
+TT = [k >= T0 for k in range(16)]
+GL = [G0 <= k < G1 for k in range(16)]
 LATE = 2
 VC = (1, 4)
 HEAD = 7
@@ -34,7 +39,7 @@ def tile_phiaslossengine_pb_kernel(tc, ag_diff, tension, hiddens, W_io, w_it, W_
         grp = ctx.enter_context(tc.tile_pool(name="grp", bufs=4))
         work = ctx.enter_context(tc.tile_pool(name="work", bufs=4))
         small = ctx.enter_context(tc.tile_pool(name="small", bufs=4))
-        outp = ctx.enter_context(tc.tile_pool(name="outp", bufs=4))
+        outp = ctx.enter_context(tc.tile_pool(name="outp", bufs=8))
         psum = ctx.enter_context(tc.psum_pool(name="psum", bufs=1))
         ctx.enter_context(tc.manual_schedule())
 
@@ -44,6 +49,7 @@ def tile_phiaslossengine_pb_kernel(tc, ag_diff, tension, hiddens, W_io, w_it, W_
         vec = const.tile([P, 36], F32, name="vec")
         brz = const.tile([P, 8], F32, name="brz")
         warm = const.tile([P, 2], F32, name="warm")
+        trow = const.tile([P, CELLS + HID], BF16, name="trow")
         tb = const.tile([P, CELLS], BF16, name="tb")
         raw = {
             "a": const.tile([P, CELLS // P, HID], BF16, name="a_raw"),
@@ -72,6 +78,7 @@ def tile_phiaslossengine_pb_kernel(tc, ag_diff, tension, hiddens, W_io, w_it, W_
 
         nc.vector.memset(warm[:, 0:1], 0.0)
         nc.vector.memset(vrows[:], 0.0)
+        nc.vector.memset(trow[:].bitcast(U32), 0)
         nc.scalar.activation(out=warm[:, 1:2], in_=warm[:, 0:1], func=ACT.Sigmoid)
 
         banks = []
@@ -95,6 +102,8 @@ def tile_phiaslossengine_pb_kernel(tc, ag_diff, tension, hiddens, W_io, w_it, W_
         nc.sync.dma_start(out=vrows[0:8, 3, :].bitcast(BF16), in_=tension.rearrange("(b w) o -> b (w o)", w=2 * P))
         load_weights(0, 0)
         load_weights(0, 1)
+        nc.sync.dma_start(out=trow[0:1, 0:CELLS], in_=tension.rearrange("c o -> o c"))
+        nc.sync.dma_start(out=trow[0:1, CELLS : CELLS + HID], in_=w_it[2 * HID : 3 * HID].rearrange("(o j) -> o j", o=1))
         for c0 in range(RANGE, CELLS, RANGE):
             load_cells(c0)
         load_weights(1, 0)
@@ -186,16 +195,25 @@ def tile_phiaslossengine_pb_kernel(tc, ag_diff, tension, hiddens, W_io, w_it, W_
                 stop=stop,
             )
 
-        def products(k):
-            for g, nm in enumerate(("r", "z")):
-                acc = psum.tile([P, RANGE], F32, tag="b%d" % g, name="p%s%d" % (nm, k))
+        def product(k, nm):
+            acc = psum.tile([P, RANGE], F32, tag="b%d" % ("r", "z", "in", "hn").index(nm), name="p%s%d" % (nm, k))
+            if nm in ("r", "z"):
+                g = ("r", "z").index(nm)
                 mx_pass(acc, 0, g, k, True, False)
                 mx_pass(acc, 1, g, k, False, True)
-                st[(nm, k)] = acc
-            for m, nm in enumerate(("in", "hn")):
-                acc = psum.tile([P, RANGE], F32, tag="b%d" % (2 + m), name="p%s%d" % (nm, k))
-                mx_pass(acc, m, 2, k, True, True)
-                st[(nm, k)] = acc
+            else:
+                mx_pass(acc, ("in", "hn").index(nm), 2, k, True, True)
+            st[(nm, k)] = acc
+
+        def outer(k):
+            c0, u, e = units[k]
+            acc = psum.tile([P, RANGE], F32, tag="b6", name="pt%d" % k)
+            nc.tensor.matmul(out=acc[:], lhsT=trow[:, CELLS + u * FAC + e : CELLS + (u + 1) * FAC : 2], rhs=trow[:, c0 : c0 + RANGE], start=True, stop=True)
+            st[("t", k)] = acc
+
+        def add_bank(k, nm):
+            t = st[("aa", k)]
+            nc.vector.tensor_tensor(out=t[:], in0=t[:], in1=st[(nm, k)][:], op=ALU.add)
 
         def add_tension(k, g, src, dst):
             c0, u, e = units[k]
@@ -246,7 +264,7 @@ def tile_phiaslossengine_pb_kernel(tc, ag_diff, tension, hiddens, W_io, w_it, W_
         def times_z(k):
             t = st[("dd", k)]
             if ZS[k]:
-                nc.vector.tensor_tensor(out=t[:], in0=t[:], in1=st[("zp", k)][:], op=ALU.mult)
+                (nc.gpsimd if GL[k] else nc.vector).tensor_tensor(out=t[:], in0=t[:], in1=st[("zp", k)][:], op=ALU.mult)
                 return
             se = small.tile([P, 2], F32, tag="se", name="se%d" % k)
             for f in range(2):
@@ -278,11 +296,16 @@ def tile_phiaslossengine_pb_kernel(tc, ag_diff, tension, hiddens, W_io, w_it, W_
                 nc.gpsimd.tensor_scalar(out=fm[:, fc], in0=fs[:, fc], scalar1=KAPPA, scalar2=0.0, op0=ALU.mult, op1=ALU.add)
             st[("fm", k)] = fm
 
+        def fin_bank(c0, u, f):
+            if u == 0:
+                return 4 + f
+            return (4, 5, 7)[(2 * (c0 // RANGE) + f) % 3]
+
         def transpose_back(k):
             c0, u, e = units[k]
             for f in range(2):
                 if e == 0:
-                    st[("fin", c0, u, f)] = psum.tile([P, 2, 2, P], F32, tag="b%d" % (4 + f + 2 * (u * c0 // RANGE % 2)), name="fin%d_%d" % (k, f))
+                    st[("fin", c0, u, f)] = psum.tile([P, 2, 2, P], F32, tag="b%d" % fin_bank(c0, u, f), name="fin%d_%d" % (k, f))
                 bank = st[("fin", c0, u, f)]
                 for t in range(2):
                     cs = slice((2 * f + t) * P, (2 * f + t + 1) * P)
@@ -339,45 +362,93 @@ def tile_phiaslossengine_pb_kernel(tc, ag_diff, tension, hiddens, W_io, w_it, W_
             bank_transpose(i, ring4(i))
             bank_copy(i, "scalar")
         bank_quantise(HEAD - 1)
-        products(0)
+        for nm in ("r", "z", "in", "hn"):
+            product(0, nm)
         wave_transpose(1)
 
-        for k in range(NU + 5):
-            if on(k):
-                add_tension(k, 0, "r", "rp")
-                add_tension(k, 1, "z", "zp")
-                sigmoid(k, 0, "rp")
-                sigmoid(k, 1, "zp")
+        def back_of(k):
+            return [j for j in range(NU) if j + (4 if GL[j] else 3) == k]
+
+        def store_of(k):
+            return [j + 1 for j in range(0, NU, 2) if max(j + 1 + (4 if GL[j + 1] else 3), j + (4 if GL[j] else 3)) + 1 == k]
+
+        for k in range(NU):
+            if on(k - 2) and GL[k - 2]:
+                h_minus_n(k - 2)
+                times_z(k - 2)
+            add_tension(k, 0, "r", "rp")
+            sigmoid(k, 0, "rp")
+            if on(k - 1) and TT[k - 1]:
+                add_bank(k - 1, "in")
+            add_tension(k, 1, "z", "zp")
+            if on(k - 3) and GL[k - 3]:
+                sum_zd(k - 3)
+                faction_term(k - 3)
+            sigmoid(k, 1, "zp")
+            if on(k - 1) and TT[k - 1]:
+                add_bank(k - 1, "t")
+            if not TT[k]:
                 add_tension(k, 2, "in", "cc")
             for i in wave(k):
                 bank_quantise(i)
-            if on(k - 1) and k < NU:
-                add_in(k - 1)
+            if on(k - 1):
+                if not TT[k - 1]:
+                    add_in(k - 1)
                 candidate(k - 1)
-            if k == NU + 1:
-                store(k - 4, (0,))
-                times_z(k - 2)
-                faction_term(k - 2)
-                store(k - 4, (1,))
-            elif on(k - 4) and units[k - 4][2] == 1:
-                store(k - 4)
+            for j in store_of(k):
+                store(j)
             for i in wave(k + 1):
                 bank_copy(i, "scalar")
-            if on(k):
-                reset_times_hn(k)
-            if on(k - 2) and k <= NU:
+            reset_times_hn(k)
+            if on(k - 2) and not GL[k - 2]:
                 times_z(k - 2)
-            if k == NU - 1:
-                add_in(k)
-                candidate(k)
-            if on(k - 2) and ZS[k - 2]:
-                sum_zd(k - 2)
-            if on(k - 1):
+                if ZS[k - 2]:
+                    sum_zd(k - 2)
+            if on(k - 1) and not GL[k - 1] and k < NU - 1:
                 h_minus_n(k - 1)
-            if on(k - 2) and k <= NU:
+            if on(k - 2) and not GL[k - 2]:
                 faction_term(k - 2)
             if on(k + 1):
-                products(k + 1)
-            if on(k - 3):
-                transpose_back(k - 3)
+                product(k + 1, "r")
+                product(k + 1, "z")
+            if TT[k]:
+                product(k, "in")
+                outer(k)
+            if on(k + 1):
+                if not TT[k + 1]:
+                    product(k + 1, "in")
+                product(k + 1, "hn")
+            for j in back_of(k):
+                transpose_back(j)
             wave_transpose(k + 2)
+
+        L = NU - 1
+        for j in store_of(NU):
+            store(j)
+        add_bank(L, "in")
+        h_minus_n(L - 1)
+        add_bank(L, "t")
+        candidate(L)
+        times_z(L - 1)
+        for j in range(NU):
+            if GL[j] and j + 3 >= NU:
+                sum_zd(j)
+                faction_term(j)
+        faction_term(L - 1)
+        h_minus_n(L)
+        for j in back_of(NU):
+            transpose_back(j)
+        for j in store_of(NU + 1):
+            store(j, (0,))
+        times_z(L)
+        faction_term(L)
+        for j in back_of(NU + 1):
+            transpose_back(j)
+        for j in store_of(NU + 1):
+            store(j, (1,))
+        for j in back_of(NU + 2):
+            transpose_back(j)
+        for j in store_of(NU + 2):
+            store(j)
+        for j in store_of(NU + 3):
+            store(j)

@@ -19,6 +19,9 @@ RANGE = 512
 GATES = 3
 FLOPS = 2 * 2 * CELLS * HID * GATES * HID
 KAPPA = 0.15 / (0.85 * FAC)
+SPLIT = True
+FA = True
+HL = False
 T0 = 6
 G0 = 6
 G1 = 13
@@ -50,6 +53,7 @@ def tile_phiaslossengine_pb_kernel(tc, ag_diff, tension, hiddens, W_io, w_it, W_
         brz = const.tile([P, 8], F32, name="brz")
         warm = const.tile([P, 2], F32, name="warm")
         trow = const.tile([P, CELLS + HID], BF16, name="trow")
+        wrow = const.tile([P, 2, 2, P], BF16, name="wrow")
         tb = const.tile([P, CELLS], BF16, name="tb")
         raw = {
             "a": const.tile([P, CELLS // P, HID], BF16, name="a_raw"),
@@ -208,7 +212,7 @@ def tile_phiaslossengine_pb_kernel(tc, ag_diff, tension, hiddens, W_io, w_it, W_
         def outer(k):
             c0, u, e = units[k]
             acc = psum.tile([P, RANGE], F32, tag="b6", name="pt%d" % k)
-            nc.tensor.matmul(out=acc[:], lhsT=trow[:, CELLS + u * FAC + e : CELLS + (u + 1) * FAC : 2], rhs=trow[:, c0 : c0 + RANGE], start=True, stop=True)
+            nc.tensor.matmul(out=acc[:], lhsT=wrow[:, u, e, :], rhs=trow[:, c0 : c0 + RANGE], start=True, stop=True)
             st[("t", k)] = acc
 
         def add_bank(k, nm):
@@ -279,19 +283,24 @@ def tile_phiaslossengine_pb_kernel(tc, ag_diff, tension, hiddens, W_io, w_it, W_
             se = small.tile([P, 2], F32, tag="se", name="se%d" % k)
             for f in range(2):
                 cs = slice(f * FAC, (f + 1) * FAC)
-                nc.scalar.activation(out=st[("zp", k)][:, cs], in_=st[("dd", k)][:, cs], func=ACT.Identity, bias=0.0, scale=1.0, accum_out=se[:, f : f + 1])
+                nc.scalar.activation(out=st[("zp", k)][:, cs], in_=st[("dd", k)][:, cs], func=ACT.Identity, bias=0.0, scale=KAPPA if GL[k] else 1.0, accum_out=se[:, f : f + 1])
             st[("se", k)] = se
 
         def faction_term(k):
             fs = small.tile([P, 2], F32, tag="fs", name="fs%d" % k)
             fm = small.tile([P, 2], F32, tag="fm", name="fm%d" % k)
-            if k >= FMS:
+            if GL[k] and FA:
+                for f in range(2):
+                    nc.scalar.activation(
+                        out=fm[:, f : f + 1], in_=st[("sn", k)][:, f : f + 1], func=ACT.Identity, scale=KAPPA, bias=st[("se", k)][:, f : f + 1]
+                    )
+            elif k >= FMS:
                 nc.scalar.mul(out=fs[:], in_=st[("sn", k)][:], mul=KAPPA)
                 for f in range(2):
                     nc.scalar.activation(
                         out=fm[:, f : f + 1], in_=st[("se", k)][:, f : f + 1], func=ACT.Identity, scale=KAPPA, bias=fs[:, f : f + 1]
                     )
-            for fc in [slice(0, 2)] if k < FMS else []:
+            for fc in [slice(0, 2)] if k < FMS and not (GL[k] and FA) else []:
                 nc.gpsimd.tensor_tensor(out=fs[:, fc], in0=st[("sn", k)][:, fc], in1=st[("se", k)][:, fc], op=ALU.add)
                 nc.gpsimd.tensor_scalar(out=fm[:, fc], in0=fs[:, fc], scalar1=KAPPA, scalar2=0.0, op0=ALU.mult, op1=ALU.add)
             st[("fm", k)] = fm
@@ -372,6 +381,16 @@ def tile_phiaslossengine_pb_kernel(tc, ag_diff, tension, hiddens, W_io, w_it, W_
         def store_of(k):
             return [j + 1 for j in range(0, NU, 2) if max(j + 1 + (4 if GL[j + 1] else 3), j + (4 if GL[j] else 3)) + 1 == k]
 
+        def stores(k):
+            r = []
+            for f in range(2):
+                for kk in (k, k - 1):
+                    for j in store_of(kk):
+                        late = SPLIT and f == 1 and j > 7 and kk + 1 < NU
+                        if kk + (1 if late else 0) == k:
+                            r.append((j, f))
+            return r
+
         for k in range(NU):
             if on(k - 2) and GL[k - 2]:
                 h_minus_n(k - 2)
@@ -383,7 +402,6 @@ def tile_phiaslossengine_pb_kernel(tc, ag_diff, tension, hiddens, W_io, w_it, W_
             add_tension(k, 1, "z", "zp")
             if on(k - 3) and GL[k - 3]:
                 sum_zd(k - 3)
-                faction_term(k - 3)
             sigmoid(k, 1, "zp")
             if on(k - 1) and TT[k - 1]:
                 add_bank(k - 1, "t")
@@ -395,10 +413,14 @@ def tile_phiaslossengine_pb_kernel(tc, ag_diff, tension, hiddens, W_io, w_it, W_
                 if not TT[k - 1]:
                     add_in(k - 1)
                 candidate(k - 1)
-            for j in store_of(k):
-                store(j)
+            if on(k - 3) and GL[k - 3]:
+                faction_term(k - 3)
+            for j, f in stores(k):
+                store(j, (f,))
             for i in wave(k + 1):
                 bank_copy(i, "scalar")
+            if k == 3:
+                nc.scalar.copy(out=wrow[:], in_=trow[:, CELLS : CELLS + HID].rearrange("p (u m e) -> p u e m", u=2, e=2))
             reset_times_hn(k)
             if on(k - 2) and not GL[k - 2]:
                 times_z(k - 2)
@@ -417,10 +439,13 @@ def tile_phiaslossengine_pb_kernel(tc, ag_diff, tension, hiddens, W_io, w_it, W_
             if on(k + 1):
                 if not TT[k + 1]:
                     product(k + 1, "in")
-                product(k + 1, "hn")
+                if not (HL and TT[k]):
+                    product(k + 1, "hn")
             for j in back_of(k):
                 transpose_back(j)
             wave_transpose(k + 2)
+            if on(k + 1) and HL and TT[k]:
+                product(k + 1, "hn")
 
         L = NU - 1
         for j in store_of(NU):

@@ -20,12 +20,13 @@ GATES = 3
 FLOPS = 2 * 2 * CELLS * HID * GATES * HID
 KAPPA = 0.15 / (0.85 * FAC)
 SPLIT = True
+FB = True
 FA = True
 HL = False
 T0 = 6
 G0 = 6
 G1 = 13
-ZS = [3 < k < 13 for k in range(16)]
+ZS = [k < 13 for k in range(16)]
 FMS = 13
 VST = 13
 TT = [k >= T0 for k in range(16)]
@@ -52,6 +53,7 @@ def tile_phiaslossengine_pb_kernel(tc, ag_diff, tension, hiddens, W_io, w_it, W_
         vec = const.tile([P, 36], F32, name="vec")
         brz = const.tile([P, 8], F32, name="brz")
         warm = const.tile([P, 2], F32, name="warm")
+        zero = const.tile([P, RANGE], BF16, name="zero")
         trow = const.tile([P, CELLS + HID], BF16, name="trow")
         wrow = const.tile([P, 2, 2, P], BF16, name="wrow")
         tb = const.tile([P, CELLS], BF16, name="tb")
@@ -80,6 +82,7 @@ def tile_phiaslossengine_pb_kernel(tc, ag_diff, tension, hiddens, W_io, w_it, W_
         units = [(c0, u, e) for u in range(2) for c0 in range(0, CELLS, RANGE) for e in range(2)]
         NU = len(units)
 
+        nc.vector.memset(zero[:], 0.0)
         nc.vector.memset(warm[:, 0:1], 0.0)
         nc.vector.memset(vrows[:], 0.0)
         nc.vector.memset(trow[:].bitcast(U32), 0)
@@ -283,13 +286,13 @@ def tile_phiaslossengine_pb_kernel(tc, ag_diff, tension, hiddens, W_io, w_it, W_
             se = small.tile([P, 2], F32, tag="se", name="se%d" % k)
             for f in range(2):
                 cs = slice(f * FAC, (f + 1) * FAC)
-                nc.scalar.activation(out=st[("zp", k)][:, cs], in_=st[("dd", k)][:, cs], func=ACT.Identity, bias=0.0, scale=KAPPA if GL[k] else 1.0, accum_out=se[:, f : f + 1])
+                nc.scalar.activation(out=st[("zp", k)][:, cs], in_=st[("dd", k)][:, cs], func=ACT.Identity, bias=0.0, scale=KAPPA if GL[k] or FB and ZS[k] else 1.0, accum_out=se[:, f : f + 1])
             st[("se", k)] = se
 
         def faction_term(k):
             fs = small.tile([P, 2], F32, tag="fs", name="fs%d" % k)
             fm = small.tile([P, 2], F32, tag="fm", name="fm%d" % k)
-            if GL[k] and FA:
+            if (GL[k] or FB and ZS[k]) and FA:
                 for f in range(2):
                     nc.scalar.activation(
                         out=fm[:, f : f + 1], in_=st[("sn", k)][:, f : f + 1], func=ACT.Identity, scale=KAPPA, bias=st[("se", k)][:, f : f + 1]
@@ -300,7 +303,7 @@ def tile_phiaslossengine_pb_kernel(tc, ag_diff, tension, hiddens, W_io, w_it, W_
                     nc.scalar.activation(
                         out=fm[:, f : f + 1], in_=st[("se", k)][:, f : f + 1], func=ACT.Identity, scale=KAPPA, bias=fs[:, f : f + 1]
                     )
-            for fc in [slice(0, 2)] if k < FMS and not (GL[k] and FA) else []:
+            for fc in [slice(0, 2)] if k < FMS and not ((GL[k] or FB and ZS[k]) and FA) else []:
                 nc.gpsimd.tensor_tensor(out=fs[:, fc], in0=st[("sn", k)][:, fc], in1=st[("se", k)][:, fc], op=ALU.add)
                 nc.gpsimd.tensor_scalar(out=fm[:, fc], in0=fs[:, fc], scalar1=KAPPA, scalar2=0.0, op0=ALU.mult, op1=ALU.add)
             st[("fm", k)] = fm
@@ -358,6 +361,12 @@ def tile_phiaslossengine_pb_kernel(tc, ag_diff, tension, hiddens, W_io, w_it, W_
         def ring4(i):
             return "b%d" % (4 + i % 4)
 
+        def warm_up(n):
+            for x in range(n):
+                acc = psum.tile([P, RANGE], F32, tag="b3", name="zz%d" % x)
+                nc.tensor.matmul(out=acc[:], lhsT=zero[:, 0:P], rhs=zero[:], start=True, stop=True)
+
+        warm_up(4)
         for i in range(HEAD):
             if i == 4:
                 spread_vectors("b0")
@@ -413,7 +422,7 @@ def tile_phiaslossengine_pb_kernel(tc, ag_diff, tension, hiddens, W_io, w_it, W_
                 if not TT[k - 1]:
                     add_in(k - 1)
                 candidate(k - 1)
-            if on(k - 3) and GL[k - 3]:
+            if on(k - 3) and ZS[k - 3]:
                 faction_term(k - 3)
             for j, f in stores(k):
                 store(j, (f,))
@@ -428,13 +437,15 @@ def tile_phiaslossengine_pb_kernel(tc, ag_diff, tension, hiddens, W_io, w_it, W_
                     sum_zd(k - 2)
             if on(k - 1) and not GL[k - 1] and k < NU - 1:
                 h_minus_n(k - 1)
-            if on(k - 2) and not GL[k - 2]:
+            if on(k - 2) and not GL[k - 2] and not ZS[k - 2]:
                 faction_term(k - 2)
             if on(k + 1):
                 product(k + 1, "r")
-                product(k + 1, "z")
             if TT[k]:
                 product(k, "in")
+            if on(k + 1):
+                product(k + 1, "z")
+            if TT[k]:
                 outer(k)
             if on(k + 1):
                 if not TT[k + 1]:

@@ -20,6 +20,7 @@ GATES = 3
 FLOPS = 2 * 2 * CELLS * HID * GATES * HID
 KAPPA = 0.15 / (0.85 * FAC)
 SPLIT = True
+LS = True
 FB = True
 FA = True
 HL = False
@@ -41,9 +42,9 @@ def tile_phiaslossengine_pb_kernel(tc, ag_diff, tension, hiddens, W_io, w_it, W_
     with ExitStack() as ctx:
         const = ctx.enter_context(tc.tile_pool(name="const", bufs=1))
         grp = ctx.enter_context(tc.tile_pool(name="grp", bufs=4))
-        work = ctx.enter_context(tc.tile_pool(name="work", bufs=4))
+        work = ctx.enter_context(tc.tile_pool(name="work", bufs=6))
         small = ctx.enter_context(tc.tile_pool(name="small", bufs=4))
-        outp = ctx.enter_context(tc.tile_pool(name="outp", bufs=8))
+        outp = ctx.enter_context(tc.tile_pool(name="outp", bufs=6))
         psum = ctx.enter_context(tc.psum_pool(name="psum", bufs=1))
         ctx.enter_context(tc.manual_schedule())
 
@@ -265,7 +266,12 @@ def tile_phiaslossengine_pb_kernel(tc, ag_diff, tension, hiddens, W_io, w_it, W_
             c0, u, e = units[k]
             t = work.tile([P, RANGE], F32, tag="dd", name="dd%d" % k)
             engine = nc.gpsimd if k < NU - LATE else nc.vector
-            engine.tensor_tensor(out=t[:], in0=ghv[:, c0 : c0 + RANGE, 2 * u + e], in1=st[("nn", k)][:], op=ALU.subtract)
+            n = 2 if k == NU - 1 else 1
+            for f in range(n):
+                a, b = f * RANGE // n, (f + 1) * RANGE // n
+                engine.tensor_tensor(
+                    out=t[:, a:b], in0=ghv[:, c0 + a : c0 + b, 2 * u + e], in1=st[("nn", k)][:, a:b], op=ALU.subtract
+                )
             st[("dd", k)] = t
 
         def times_z(k):
@@ -282,11 +288,13 @@ def tile_phiaslossengine_pb_kernel(tc, ag_diff, tension, hiddens, W_io, w_it, W_
                 )
             st[("se", k)] = se
 
+        junk = const.tile([P, RANGE], F32, name="junk")
+
         def sum_zd(k):
             se = small.tile([P, 2], F32, tag="se", name="se%d" % k)
             for f in range(2):
                 cs = slice(f * FAC, (f + 1) * FAC)
-                nc.scalar.activation(out=st[("zp", k)][:, cs], in_=st[("dd", k)][:, cs], func=ACT.Identity, bias=0.0, scale=KAPPA if GL[k] or FB and ZS[k] else 1.0, accum_out=se[:, f : f + 1])
+                nc.scalar.activation(out=junk[:, cs], in_=st[("dd", k)][:, cs], func=ACT.Identity, bias=0.0, scale=KAPPA if GL[k] or FB and ZS[k] else 1.0, accum_out=se[:, f : f + 1])
             st[("se", k)] = se
 
         def faction_term(k):
@@ -313,30 +321,46 @@ def tile_phiaslossengine_pb_kernel(tc, ag_diff, tension, hiddens, W_io, w_it, W_
                 return 4 + f
             return (4, 5, 7)[(2 * (c0 // RANGE) + f) % 3]
 
-        def transpose_back(k):
+        def transpose_back(k, factions=(0, 1)):
             c0, u, e = units[k]
-            for f in range(2):
+            for f in factions:
                 if e == 0:
-                    st[("fin", c0, u, f)] = psum.tile([P, 2, 2, P], F32, tag="b%d" % fin_bank(c0, u, f), name="fin%d_%d" % (k, f))
-                bank = st[("fin", c0, u, f)]
+                    if LS and k == NU - 2 and f == 1:
+                        st[("fin", c0, u, f)] = [psum.tile([P, 1, 2, P], F32, tag="b%d" % t, name="fin%d_%d_%d" % (k, f, t)) for t in range(2)]
+                    else:
+                        st[("fin", c0, u, f)] = psum.tile([P, 2, 2, P], F32, tag="b%d" % fin_bank(c0, u, f), name="fin%d_%d" % (k, f))
                 for t in range(2):
+                    bank = st[("fin", c0, u, f)]
+                    if LS and k >= NU - 2 and f == 1:
+                        bank = bank[t][:]
+                    else:
+                        bank = bank[:, t : t + 1]
                     cs = slice((2 * f + t) * P, (2 * f + t + 1) * P)
                     terms = (st[("nn", k)][:, cs], st[("dd", k)][:, cs], st[("fm", k)][:, f : f + 1].to_broadcast([P, P]))
                     for x, term in enumerate(terms):
                         nc.tensor.matmul(
-                            out=bank[:, t, e, :], lhsT=term, rhs=ident[:], is_transpose=True, start=(x == 0), stop=(x == 2)
+                            out=bank[:, 0, e, :], lhsT=term, rhs=ident[:], is_transpose=True, start=(x == 0), stop=(x == 2)
                         )
 
         def store(k, factions=(0, 1)):
             c0, u, e = units[k]
             for f in factions:
                 o = outp.tile([P, 2, P, 2], F32, tag="osb", name="osb%d_%d" % (k, f))
+                t0 = c0 // P + 2 * f
+                if LS and k == NU - 1 and f == 1:
+                    for t in range(2):
+                        src = st[("fin", c0, u, f)][t][:].rearrange("c t e p -> c t p e")
+                        if t == 0:
+                            nc.vector.tensor_scalar(out=o[:, 0:1], in0=src, scalar1=0.85, scalar2=0.0, op0=ALU.mult, op1=ALU.add)
+                        else:
+                            nc.scalar.mul(out=o[:, 1:2], in_=src, mul=0.85)
+                        nc.sync.dma_start(out=oview[:, t0 + t : t0 + t + 1, u * FAC : (u + 1) * FAC], in_=o[:, t : t + 1].rearrange("c t p e -> c t (p e)"))
+                    continue
                 src = st[("fin", c0, u, f)][:].rearrange("c t e p -> c t p e")
                 if k >= VST and f == 1:
                     nc.vector.tensor_scalar(out=o[:], in0=src, scalar1=0.85, scalar2=0.0, op0=ALU.mult, op1=ALU.add)
                 else:
                     nc.scalar.mul(out=o[:], in_=src, mul=0.85)
-                t0 = c0 // P + 2 * f
                 nc.sync.dma_start(out=oview[:, t0 : t0 + 2, u * FAC : (u + 1) * FAC], in_=o[:].rearrange("c t p e -> c t (p e)"))
 
         rest = list(range(HEAD, len(banks)))
@@ -380,7 +404,7 @@ def tile_phiaslossengine_pb_kernel(tc, ag_diff, tension, hiddens, W_io, w_it, W_
             bank_transpose(i, ring4(i))
             bank_copy(i, "scalar")
         bank_quantise(HEAD - 1)
-        for nm in ("r", "z", "in", "hn"):
+        for nm in ("r", "z", "hn", "in"):
             product(0, nm)
         wave_transpose(1)
 
@@ -445,13 +469,13 @@ def tile_phiaslossengine_pb_kernel(tc, ag_diff, tension, hiddens, W_io, w_it, W_
                 product(k, "in")
             if on(k + 1):
                 product(k + 1, "z")
-            if TT[k]:
-                outer(k)
             if on(k + 1):
-                if not TT[k + 1]:
-                    product(k + 1, "in")
                 if not (HL and TT[k]):
                     product(k + 1, "hn")
+                if not TT[k + 1]:
+                    product(k + 1, "in")
+            if TT[k]:
+                outer(k)
             for j in back_of(k):
                 transpose_back(j)
             wave_transpose(k + 2)
@@ -472,8 +496,9 @@ def tile_phiaslossengine_pb_kernel(tc, ag_diff, tension, hiddens, W_io, w_it, W_
                 faction_term(j)
         faction_term(L - 1)
         h_minus_n(L)
-        for j in back_of(NU):
-            transpose_back(j)
+        for f in range(2):
+            for j in back_of(NU):
+                transpose_back(j, (f,))
         for j in store_of(NU + 1):
             store(j, (0,))
         times_z(L)

@@ -21,11 +21,13 @@ FLOPS = 2 * 2 * CELLS * HID * GATES * HID
 KAPPA = 0.15 / (0.85 * FAC)
 SPLIT = True
 LS = True
+FB3 = (4, 5, 7)
+QL = 5
 FB = True
 FA = True
 HL = False
-T0 = 6
-G0 = 6
+T0 = 5
+G0 = 5
 G1 = 13
 ZS = [k < 13 for k in range(16)]
 FMS = 13
@@ -319,7 +321,7 @@ def tile_phiaslossengine_pb_kernel(tc, ag_diff, tension, hiddens, W_io, w_it, W_
         def fin_bank(c0, u, f):
             if u == 0:
                 return 4 + f
-            return (4, 5, 7)[(2 * (c0 // RANGE) + f) % 3]
+            return FB3[(2 * (c0 // RANGE) + f) % len(FB3)]
 
         def transpose_back(k, factions=(0, 1)):
             c0, u, e = units[k]
@@ -336,7 +338,7 @@ def tile_phiaslossengine_pb_kernel(tc, ag_diff, tension, hiddens, W_io, w_it, W_
                     else:
                         bank = bank[:, t : t + 1]
                     cs = slice((2 * f + t) * P, (2 * f + t + 1) * P)
-                    terms = (st[("nn", k)][:, cs], st[("dd", k)][:, cs], st[("fm", k)][:, f : f + 1].to_broadcast([P, P]))
+                    terms = (st[("fm", k)][:, f : f + 1].to_broadcast([P, P]), st[("nn", k)][:, cs], st[("dd", k)][:, cs])
                     for x, term in enumerate(terms):
                         nc.tensor.matmul(
                             out=bank[:, 0, e, :], lhsT=term, rhs=ident[:], is_transpose=True, start=(x == 0), stop=(x == 2)
@@ -364,7 +366,7 @@ def tile_phiaslossengine_pb_kernel(tc, ag_diff, tension, hiddens, W_io, w_it, W_
                 nc.sync.dma_start(out=oview[:, t0 : t0 + 2, u * FAC : (u + 1) * FAC], in_=o[:].rearrange("c t p e -> c t (p e)"))
 
         rest = list(range(HEAD, len(banks)))
-        waves = [rest[0:3], rest[3:7], rest[7:11]] + [rest[i : i + 2] for i in range(11, len(rest), 2)]
+        waves = [rest[0:3], rest[3:7], rest[7:11], rest[11:15], rest[15:17]] + [rest[i : i + 1] for i in range(17, len(rest))]
         second = set()
         for wv in waves:
             second.update(wv[1::2])
@@ -374,7 +376,7 @@ def tile_phiaslossengine_pb_kernel(tc, ag_diff, tension, hiddens, W_io, w_it, W_
 
         def wave_transpose(w):
             for i in wave(w):
-                bank_transpose(i, ring4(i) if w < 3 else "b%d" % (6 + i % 2))
+                bank_transpose(i, ring4(i) if w < 4 else "b%d" % (6 + i % 2) if w == 4 else "b7")
 
         def on(k):
             return 0 <= k < NU
@@ -440,8 +442,9 @@ def tile_phiaslossengine_pb_kernel(tc, ag_diff, tension, hiddens, W_io, w_it, W_
                 add_bank(k - 1, "t")
             if not TT[k]:
                 add_tension(k, 2, "in", "cc")
-            for i in wave(k):
-                bank_quantise(i)
+            if k < QL:
+                for i in wave(k):
+                    bank_quantise(i)
             if on(k - 1):
                 if not TT[k - 1]:
                     add_in(k - 1)
@@ -455,6 +458,9 @@ def tile_phiaslossengine_pb_kernel(tc, ag_diff, tension, hiddens, W_io, w_it, W_
             if k == 3:
                 nc.scalar.copy(out=wrow[:], in_=trow[:, CELLS : CELLS + HID].rearrange("p (u m e) -> p u e m", u=2, e=2))
             reset_times_hn(k)
+            if k >= QL:
+                for i in wave(k):
+                    bank_quantise(i)
             if on(k - 2) and not GL[k - 2]:
                 times_z(k - 2)
                 if ZS[k - 2]:

@@ -18,25 +18,14 @@ FAC = 256
 RANGE = 512
 GATES = 3
 FLOPS = 2 * 2 * CELLS * HID * GATES * HID
-KAPPA = 0.15 / (0.85 * FAC)
-SPLIT = True
-LS = True
-FB3 = (4, 5, 7)
-QL = 5
-FB = True
-FA = True
-HL = False
-T0 = 5
-G0 = 5
-G1 = 13
-ZS = [k < 13 for k in range(16)]
-FMS = 13
-VST = 13
-TT = [k >= T0 for k in range(16)]
-GL = [G0 <= k < G1 for k in range(16)]
-LATE = 2
-VC = (1, 4)
+BLEND = 0.85
+KAPPA = 0.15 / (BLEND * FAC)
+
+LONG = range(5, 13)
+LAST = 2
 HEAD = 7
+HEAD_ON_VECTOR = (1, 4)
+WARM = 4
 
 
 def tile_phiaslossengine_pb_kernel(tc, ag_diff, tension, hiddens, W_io, w_it, W_hh, b_ih, b_hh, out):
@@ -55,8 +44,9 @@ def tile_phiaslossengine_pb_kernel(tc, ag_diff, tension, hiddens, W_io, w_it, W_
         vrows = const.tile([P, 4, P], F32, name="vrows")
         vec = const.tile([P, 36], F32, name="vec")
         brz = const.tile([P, 8], F32, name="brz")
-        warm = const.tile([P, 2], F32, name="warm")
+        table = const.tile([P, 2], F32, name="table")
         zero = const.tile([P, RANGE], BF16, name="zero")
+        junk = const.tile([P, RANGE], F32, name="junk")
         trow = const.tile([P, CELLS + HID], BF16, name="trow")
         wrow = const.tile([P, 2, 2, P], BF16, name="wrow")
         tb = const.tile([P, CELLS], BF16, name="tb")
@@ -86,17 +76,17 @@ def tile_phiaslossengine_pb_kernel(tc, ag_diff, tension, hiddens, W_io, w_it, W_
         NU = len(units)
 
         nc.vector.memset(zero[:], 0.0)
-        nc.vector.memset(warm[:, 0:1], 0.0)
+        nc.vector.memset(table[:, 0:1], 0.0)
         nc.vector.memset(vrows[:], 0.0)
         nc.vector.memset(trow[:].bitcast(U32), 0)
-        nc.scalar.activation(out=warm[:, 1:2], in_=warm[:, 0:1], func=ACT.Sigmoid)
+        nc.scalar.activation(out=table[:, 1:2], in_=table[:, 0:1], func=ACT.Sigmoid)
 
         banks = []
 
         def load_cells(c0):
             t0 = c0 // P
+            piece = FAC // P if c0 == 0 else RANGE // P
             for nm in ("a", "h"):
-                piece = FAC // P if c0 == 0 else RANGE // P
                 for t in range(t0, t0 + RANGE // P, piece):
                     nc.sync.dma_start(out=raw[nm][:, t : t + piece, :], in_=dview[nm][:, t : t + piece, :])
                 banks.extend([(nm, f) for f in range(c0 // FAC, (c0 + RANGE) // FAC)])
@@ -122,6 +112,24 @@ def tile_phiaslossengine_pb_kernel(tc, ag_diff, tension, hiddens, W_io, w_it, W_
         make_identity(nc, ident[:])
         make_identity(nc, identb[:])
 
+        sizes = (3, 4, 4, 4, 2) + (1,) * 4
+        waves = []
+        first = HEAD
+        for size in sizes:
+            waves.append(list(range(first, first + size)))
+            first += size
+        second = set()
+        for wave in waves:
+            second.update(wave[1::2])
+
+        def wave_of(k):
+            return waves[k] if k < len(waves) else []
+
+        def wave_tag(k, i):
+            if k < 4:
+                return "b%d" % (4 + i % 4)
+            return "b%d" % (6 + i % 2) if k == 4 else "b7"
+
         st = {}
 
         def bank_transpose(i, tag):
@@ -140,12 +148,11 @@ def tile_phiaslossengine_pb_kernel(tc, ag_diff, tension, hiddens, W_io, w_it, W_
             nm, j = banks[i]
             if nm == "h":
                 g = gh[:, j]
+            elif i in second:
+                g = st[("grp", i - 1)][:, 1]
             else:
-                if i not in second:
-                    st[("grp", i)] = grp.tile([P, 2, 2, P, 4], BF16, tag="grp", name="grp%d" % i, align_bytes=64)
-                    g = st[("grp", i)][:, 0]
-                else:
-                    g = st[("grp", i - 1)][:, 1]
+                st[("grp", i)] = grp.tile([P, 2, 2, P, 4], BF16, tag="grp", name="grp%d" % i, align_bytes=64)
+                g = st[("grp", i)][:, 0]
             words = st[("xt", i)][:].rearrange("q t w r -> q t r w")
             if engine == "vector":
                 nc.vector.tensor_copy(out=g.bitcast(F32), in_=words)
@@ -164,6 +171,10 @@ def tile_phiaslossengine_pb_kernel(tc, ag_diff, tension, hiddens, W_io, w_it, W_
                 scales=scl[nm][:, cols],
                 in_=src.rearrange("q b t r j -> q (b t r j)"),
             )
+
+        def wave_transpose(k):
+            for i in wave_of(k):
+                bank_transpose(i, wave_tag(k, i))
 
         def spread_vectors(tag):
             vps = psum.tile([P, 512], F32, tag=tag, name="vps")
@@ -186,7 +197,7 @@ def tile_phiaslossengine_pb_kernel(tc, ag_diff, tension, hiddens, W_io, w_it, W_
                 )
             nc.scalar.copy(out=tb[:, half * 1024 : (half + 1) * 1024], in_=tp[:])
 
-        def vcol(v, g, k):
+        def column(v, g, k):
             c0, u, e = units[k]
             c = ((v * GATES + g) * 2 + u) * 2 + e
             return vec[:, c : c + 1]
@@ -215,21 +226,17 @@ def tile_phiaslossengine_pb_kernel(tc, ag_diff, tension, hiddens, W_io, w_it, W_
                 mx_pass(acc, ("in", "hn").index(nm), 2, k, True, True)
             st[(nm, k)] = acc
 
-        def outer(k):
+        def outer_product(k):
             c0, u, e = units[k]
             acc = psum.tile([P, RANGE], F32, tag="b6", name="pt%d" % k)
             nc.tensor.matmul(out=acc[:], lhsT=wrow[:, u, e, :], rhs=trow[:, c0 : c0 + RANGE], start=True, stop=True)
             st[("t", k)] = acc
 
-        def add_bank(k, nm):
-            t = st[("aa", k)]
-            nc.vector.tensor_tensor(out=t[:], in0=t[:], in1=st[(nm, k)][:], op=ALU.add)
-
         def add_tension(k, g, src, dst):
             c0, u, e = units[k]
             t = work.tile([P, RANGE], F32, tag=dst, name="%s%d" % (dst, k))
             nc.vector.scalar_tensor_tensor(
-                out=t[:], in0=tb[:, c0 : c0 + RANGE], scalar=vcol(0, g, k), in1=st[(src, k)][:], op0=ALU.mult, op1=ALU.add
+                out=t[:], in0=tb[:, c0 : c0 + RANGE], scalar=column(0, g, k), in1=st[(src, k)][:], op0=ALU.mult, op1=ALU.add
             )
             st[(dst, k)] = t
 
@@ -242,13 +249,13 @@ def tile_phiaslossengine_pb_kernel(tc, ag_diff, tension, hiddens, W_io, w_it, W_
         def reset_times_hn(k):
             t = work.tile([P, RANGE], F32, tag="aa", name="aa%d" % k)
             nc.vector.scalar_tensor_tensor(
-                out=t[:], in0=st[("hn", k)][:], scalar=vcol(2, 2, k), in1=st[("rp", k)][:], op0=ALU.add, op1=ALU.mult
+                out=t[:], in0=st[("hn", k)][:], scalar=column(2, 2, k), in1=st[("rp", k)][:], op0=ALU.add, op1=ALU.mult
             )
             st[("aa", k)] = t
 
-        def add_in(k):
+        def add_to_aa(k, nm):
             t = st[("aa", k)]
-            nc.vector.tensor_tensor(out=t[:], in0=t[:], in1=st[("cc", k)][:], op=ALU.add)
+            nc.vector.tensor_tensor(out=t[:], in0=t[:], in1=st[(nm, k)][:], op=ALU.add)
 
         def candidate(k):
             t = work.tile([P, RANGE], F32, tag="nn", name="nn%d" % k)
@@ -256,7 +263,7 @@ def tile_phiaslossengine_pb_kernel(tc, ag_diff, tension, hiddens, W_io, w_it, W_
             for f in range(2):
                 cs = slice(f * FAC, (f + 1) * FAC)
                 nc.scalar.activation(
-                    out=t[:, cs], in_=st[("aa", k)][:, cs], func=ACT.Tanh, bias=vcol(1, 2, k), scale=1.0,
+                    out=t[:, cs], in_=st[("aa", k)][:, cs], func=ACT.Tanh, bias=column(1, 2, k), scale=1.0,
                     accum_out=sn[:, f : f + 1],
                 )
             st[("nn", k)] = t
@@ -267,10 +274,10 @@ def tile_phiaslossengine_pb_kernel(tc, ag_diff, tension, hiddens, W_io, w_it, W_
         def h_minus_n(k):
             c0, u, e = units[k]
             t = work.tile([P, RANGE], F32, tag="dd", name="dd%d" % k)
-            engine = nc.gpsimd if k < NU - LATE else nc.vector
-            n = 2 if k == NU - 1 else 1
-            for f in range(n):
-                a, b = f * RANGE // n, (f + 1) * RANGE // n
+            engine = nc.gpsimd if k < NU - LAST else nc.vector
+            parts = 2 if k == NU - 1 else 1
+            for i in range(parts):
+                a, b = i * RANGE // parts, (i + 1) * RANGE // parts
                 engine.tensor_tensor(
                     out=t[:, a:b], in0=ghv[:, c0 + a : c0 + b, 2 * u + e], in1=st[("nn", k)][:, a:b], op=ALU.subtract
                 )
@@ -278,9 +285,30 @@ def tile_phiaslossengine_pb_kernel(tc, ag_diff, tension, hiddens, W_io, w_it, W_
 
         def times_z(k):
             t = st[("dd", k)]
-            if ZS[k]:
-                (nc.gpsimd if GL[k] else nc.vector).tensor_tensor(out=t[:], in0=t[:], in1=st[("zp", k)][:], op=ALU.mult)
-                return
+            engine = nc.gpsimd if k in LONG else nc.vector
+            engine.tensor_tensor(out=t[:], in0=t[:], in1=st[("zp", k)][:], op=ALU.mult)
+
+        def sum_zd(k):
+            se = small.tile([P, 2], F32, tag="se", name="se%d" % k)
+            for f in range(2):
+                cs = slice(f * FAC, (f + 1) * FAC)
+                nc.scalar.activation(
+                    out=junk[:, cs], in_=st[("dd", k)][:, cs], func=ACT.Identity, bias=0.0, scale=KAPPA,
+                    accum_out=se[:, f : f + 1],
+                )
+            st[("se", k)] = se
+
+        def faction_term(k):
+            fm = small.tile([P, 2], F32, tag="fm", name="fm%d" % k)
+            for f in range(2):
+                nc.scalar.activation(
+                    out=fm[:, f : f + 1], in_=st[("sn", k)][:, f : f + 1], func=ACT.Identity, scale=KAPPA,
+                    bias=st[("se", k)][:, f : f + 1],
+                )
+            st[("fm", k)] = fm
+
+        def times_z_and_sum(k):
+            t = st[("dd", k)]
             se = small.tile([P, 2], F32, tag="se", name="se%d" % k)
             for f in range(2):
                 cs = slice(f * FAC, (f + 1) * FAC)
@@ -290,232 +318,178 @@ def tile_phiaslossengine_pb_kernel(tc, ag_diff, tension, hiddens, W_io, w_it, W_
                 )
             st[("se", k)] = se
 
-        junk = const.tile([P, RANGE], F32, name="junk")
-
-        def sum_zd(k):
-            se = small.tile([P, 2], F32, tag="se", name="se%d" % k)
-            for f in range(2):
-                cs = slice(f * FAC, (f + 1) * FAC)
-                nc.scalar.activation(out=junk[:, cs], in_=st[("dd", k)][:, cs], func=ACT.Identity, bias=0.0, scale=KAPPA if GL[k] or FB and ZS[k] else 1.0, accum_out=se[:, f : f + 1])
-            st[("se", k)] = se
-
-        def faction_term(k):
-            fs = small.tile([P, 2], F32, tag="fs", name="fs%d" % k)
+        def last_faction_term(k):
+            sk = small.tile([P, 2], F32, tag="sk", name="sk%d" % k)
             fm = small.tile([P, 2], F32, tag="fm", name="fm%d" % k)
-            if (GL[k] or FB and ZS[k]) and FA:
-                for f in range(2):
-                    nc.scalar.activation(
-                        out=fm[:, f : f + 1], in_=st[("sn", k)][:, f : f + 1], func=ACT.Identity, scale=KAPPA, bias=st[("se", k)][:, f : f + 1]
-                    )
-            elif k >= FMS:
-                nc.scalar.mul(out=fs[:], in_=st[("sn", k)][:], mul=KAPPA)
-                for f in range(2):
-                    nc.scalar.activation(
-                        out=fm[:, f : f + 1], in_=st[("se", k)][:, f : f + 1], func=ACT.Identity, scale=KAPPA, bias=fs[:, f : f + 1]
-                    )
-            for fc in [slice(0, 2)] if k < FMS and not ((GL[k] or FB and ZS[k]) and FA) else []:
-                nc.gpsimd.tensor_tensor(out=fs[:, fc], in0=st[("sn", k)][:, fc], in1=st[("se", k)][:, fc], op=ALU.add)
-                nc.gpsimd.tensor_scalar(out=fm[:, fc], in0=fs[:, fc], scalar1=KAPPA, scalar2=0.0, op0=ALU.mult, op1=ALU.add)
+            nc.scalar.mul(out=sk[:], in_=st[("sn", k)][:], mul=KAPPA)
+            for f in range(2):
+                nc.scalar.activation(
+                    out=fm[:, f : f + 1], in_=st[("se", k)][:, f : f + 1], func=ACT.Identity, scale=KAPPA,
+                    bias=sk[:, f : f + 1],
+                )
             st[("fm", k)] = fm
 
-        def fin_bank(c0, u, f):
-            if u == 0:
-                return 4 + f
-            return FB3[(2 * (c0 // RANGE) + f) % len(FB3)]
+        def result_banks(k, f):
+            c0, u, e = units[k]
+            if k == NU - 2 and f == 1:
+                return [psum.tile([P, 1, 2, P], F32, tag="b%d" % t, name="fin%d_%d_%d" % (k, f, t)) for t in range(2)]
+            tag = 4 + f if u == 0 else (4, 5, 7)[(c0 // FAC + f) % 3]
+            return [psum.tile([P, 2, 2, P], F32, tag="b%d" % tag, name="fin%d_%d" % (k, f))]
 
         def transpose_back(k, factions=(0, 1)):
             c0, u, e = units[k]
             for f in factions:
                 if e == 0:
-                    if LS and k == NU - 2 and f == 1:
-                        st[("fin", c0, u, f)] = [psum.tile([P, 1, 2, P], F32, tag="b%d" % t, name="fin%d_%d_%d" % (k, f, t)) for t in range(2)]
-                    else:
-                        st[("fin", c0, u, f)] = psum.tile([P, 2, 2, P], F32, tag="b%d" % fin_bank(c0, u, f), name="fin%d_%d" % (k, f))
+                    st[("fin", c0, u, f)] = result_banks(k, f)
+                fin = st[("fin", c0, u, f)]
                 for t in range(2):
-                    bank = st[("fin", c0, u, f)]
-                    if LS and k >= NU - 2 and f == 1:
-                        bank = bank[t][:]
-                    else:
-                        bank = bank[:, t : t + 1]
+                    block = fin[t][:, 0, e, :] if len(fin) == 2 else fin[0][:, t, e, :]
                     cs = slice((2 * f + t) * P, (2 * f + t + 1) * P)
-                    terms = (st[("fm", k)][:, f : f + 1].to_broadcast([P, P]), st[("nn", k)][:, cs], st[("dd", k)][:, cs])
+                    terms = (st[("nn", k)][:, cs], st[("dd", k)][:, cs], st[("fm", k)][:, f : f + 1].to_broadcast([P, P]))
                     for x, term in enumerate(terms):
                         nc.tensor.matmul(
-                            out=bank[:, 0, e, :], lhsT=term, rhs=ident[:], is_transpose=True, start=(x == 0), stop=(x == 2)
+                            out=block, lhsT=term, rhs=ident[:], is_transpose=True, start=(x == 0), stop=(x == 2)
                         )
 
-        def store(k, factions=(0, 1)):
+        def copy_scaled(engine, o, fin):
+            src = fin[:].rearrange("c t e p -> c t p e")
+            if engine == "vector":
+                nc.vector.tensor_scalar(out=o, in0=src, scalar1=BLEND, scalar2=0.0, op0=ALU.mult, op1=ALU.add)
+            else:
+                nc.scalar.mul(out=o, in_=src, mul=BLEND)
+
+        def store(k, f):
             c0, u, e = units[k]
-            for f in factions:
-                o = outp.tile([P, 2, P, 2], F32, tag="osb", name="osb%d_%d" % (k, f))
-                t0 = c0 // P + 2 * f
-                if LS and k == NU - 1 and f == 1:
-                    for t in range(2):
-                        src = st[("fin", c0, u, f)][t][:].rearrange("c t e p -> c t p e")
-                        if t == 0:
-                            nc.vector.tensor_scalar(out=o[:, 0:1], in0=src, scalar1=0.85, scalar2=0.0, op0=ALU.mult, op1=ALU.add)
-                        else:
-                            nc.scalar.mul(out=o[:, 1:2], in_=src, mul=0.85)
-                        nc.sync.dma_start(out=oview[:, t0 + t : t0 + t + 1, u * FAC : (u + 1) * FAC], in_=o[:, t : t + 1].rearrange("c t p e -> c t (p e)"))
-                    continue
-                src = st[("fin", c0, u, f)][:].rearrange("c t e p -> c t p e")
-                if k >= VST and f == 1:
-                    nc.vector.tensor_scalar(out=o[:], in0=src, scalar1=0.85, scalar2=0.0, op0=ALU.mult, op1=ALU.add)
-                else:
-                    nc.scalar.mul(out=o[:], in_=src, mul=0.85)
-                nc.sync.dma_start(out=oview[:, t0 : t0 + 2, u * FAC : (u + 1) * FAC], in_=o[:].rearrange("c t p e -> c t (p e)"))
+            fin = st[("fin", c0, u, f)]
+            n = 2 // len(fin)
+            o = outp.tile([P, 2, P, 2], F32, tag="osb", name="osb%d_%d" % (k, f))
+            for i, bank in enumerate(fin):
+                on_vector = k >= LONG.stop and f == 1 and i == 0
+                t = i * n
+                copy_scaled("vector" if on_vector else "scalar", o[:, t : t + n], bank)
+                t0 = c0 // P + 2 * f + t
+                nc.sync.dma_start(
+                    out=oview[:, t0 : t0 + n, u * FAC : (u + 1) * FAC], in_=o[:, t : t + n].rearrange("c t p e -> c t (p e)")
+                )
 
-        rest = list(range(HEAD, len(banks)))
-        waves = [rest[0:3], rest[3:7], rest[7:11], rest[11:15], rest[15:17]] + [rest[i : i + 1] for i in range(17, len(rest))]
-        second = set()
-        for wv in waves:
-            second.update(wv[1::2])
-
-        def wave(w):
-            return waves[w] if 0 <= w < len(waves) else []
-
-        def wave_transpose(w):
-            for i in wave(w):
-                bank_transpose(i, ring4(i) if w < 4 else "b%d" % (6 + i % 2) if w == 4 else "b7")
-
-        def on(k):
-            return 0 <= k < NU
-
-        def ring8(i):
-            return "b%d" % (2 + i % 6) if i < 7 else "b%d" % (4 + i % 4)
-
-        def ring4(i):
-            return "b%d" % (4 + i % 4)
-
-        def warm_up(n):
-            for x in range(n):
-                acc = psum.tile([P, RANGE], F32, tag="b3", name="zz%d" % x)
-                nc.tensor.matmul(out=acc[:], lhsT=zero[:, 0:P], rhs=zero[:], start=True, stop=True)
-
-        warm_up(4)
+        for x in range(WARM):
+            acc = psum.tile([P, RANGE], F32, tag="b3", name="zz%d" % x)
+            nc.tensor.matmul(out=acc[:], lhsT=zero[:, 0:P], rhs=zero[:], start=True, stop=True)
         for i in range(HEAD):
-            if i == 4:
+            if i == HEAD - GATES:
                 spread_vectors("b0")
                 spread_tension(0, "b1")
                 spread_tension(1, "b0")
-            bank_transpose(i, ring8(i))
-            bank_copy(i, "vector" if i in VC else "scalar")
+            bank_transpose(i, "b%d" % (2 + i % 6))
+            bank_copy(i, "vector" if i in HEAD_ON_VECTOR else "scalar")
             if i >= 1:
                 bank_quantise(i - 1)
-        for i in wave(0):
-            bank_transpose(i, ring4(i))
+        for i in wave_of(0):
+            bank_transpose(i, wave_tag(0, i))
             bank_copy(i, "scalar")
         bank_quantise(HEAD - 1)
         for nm in ("r", "z", "hn", "in"):
             product(0, nm)
         wave_transpose(1)
 
-        def back_of(k):
-            return [j for j in range(NU) if j + (4 if GL[j] else 3) == k]
+        def back_period(k):
+            return k + (4 if k in LONG else 3)
 
-        def store_of(k):
-            return [j + 1 for j in range(0, NU, 2) if max(j + 1 + (4 if GL[j + 1] else 3), j + (4 if GL[j] else 3)) + 1 == k]
+        def backs(period):
+            return [k for k in range(NU) if back_period(k) == period]
 
-        def stores(k):
-            r = []
-            for f in range(2):
-                for kk in (k, k - 1):
-                    for j in store_of(kk):
-                        late = SPLIT and f == 1 and j > 7 and kk + 1 < NU
-                        if kk + (1 if late else 0) == k:
-                            r.append((j, f))
-            return r
+        store_period = {}
+        for k in range(1, NU, 2):
+            done = back_period(k) + 1
+            store_period[(k, 0)] = done
+            store_period[(k, 1)] = done + 1 if units[k][1] == 1 and done + 1 < NU else done
+
+        def stores(period):
+            return [key for key in store_period if store_period[key] == period]
 
         for k in range(NU):
-            if on(k - 2) and GL[k - 2]:
+            if k - 2 in LONG:
                 h_minus_n(k - 2)
                 times_z(k - 2)
             add_tension(k, 0, "r", "rp")
             sigmoid(k, 0, "rp")
-            if on(k - 1) and TT[k - 1]:
-                add_bank(k - 1, "in")
+            if k - 1 >= LONG.start:
+                add_to_aa(k - 1, "in")
             add_tension(k, 1, "z", "zp")
-            if on(k - 3) and GL[k - 3]:
+            if k - 3 in LONG:
                 sum_zd(k - 3)
             sigmoid(k, 1, "zp")
-            if on(k - 1) and TT[k - 1]:
-                add_bank(k - 1, "t")
-            if not TT[k]:
+            if k - 1 >= LONG.start:
+                add_to_aa(k - 1, "t")
+            if k < LONG.start:
                 add_tension(k, 2, "in", "cc")
-            if k < QL:
-                for i in wave(k):
+                for i in wave_of(k):
                     bank_quantise(i)
-            if on(k - 1):
-                if not TT[k - 1]:
-                    add_in(k - 1)
+            if 0 <= k - 1 < LONG.start:
+                add_to_aa(k - 1, "cc")
+            if k >= 1:
                 candidate(k - 1)
-            if on(k - 3) and ZS[k - 3]:
+            if 0 <= k - 3 < LONG.stop:
                 faction_term(k - 3)
             for j, f in stores(k):
-                store(j, (f,))
-            for i in wave(k + 1):
+                store(j, f)
+            for i in wave_of(k + 1):
                 bank_copy(i, "scalar")
-            if k == 3:
-                nc.scalar.copy(out=wrow[:], in_=trow[:, CELLS : CELLS + HID].rearrange("p (u m e) -> p u e m", u=2, e=2))
+            if k == LONG.start - 2:
+                w_n = trow[:, CELLS : CELLS + HID].rearrange("p (u m e) -> p u e m", u=2, e=2)
+                nc.scalar.copy(out=wrow[:], in_=w_n)
             reset_times_hn(k)
-            if k >= QL:
-                for i in wave(k):
+            if k >= LONG.start:
+                for i in wave_of(k):
                     bank_quantise(i)
-            if on(k - 2) and not GL[k - 2]:
+            if 0 <= k - 2 < LONG.start:
                 times_z(k - 2)
-                if ZS[k - 2]:
-                    sum_zd(k - 2)
-            if on(k - 1) and not GL[k - 1] and k < NU - 1:
+                sum_zd(k - 2)
+            if k - 2 >= LONG.stop:
+                times_z_and_sum(k - 2)
+            if 0 <= k - 1 < LONG.start or LONG.stop <= k - 1 < NU - LAST:
                 h_minus_n(k - 1)
-            if on(k - 2) and not GL[k - 2] and not ZS[k - 2]:
-                faction_term(k - 2)
-            if on(k + 1):
+            if k - 2 >= LONG.stop:
+                last_faction_term(k - 2)
+            if k + 1 < NU:
                 product(k + 1, "r")
-            if TT[k]:
+            if k >= LONG.start:
                 product(k, "in")
-            if on(k + 1):
+            if k + 1 < NU:
                 product(k + 1, "z")
-            if on(k + 1):
-                if not (HL and TT[k]):
-                    product(k + 1, "hn")
-                if not TT[k + 1]:
-                    product(k + 1, "in")
-            if TT[k]:
-                outer(k)
-            for j in back_of(k):
+                product(k + 1, "hn")
+            if k + 1 < LONG.start:
+                product(k + 1, "in")
+            if k >= LONG.start:
+                outer_product(k)
+            for j in backs(k):
                 transpose_back(j)
             wave_transpose(k + 2)
-            if on(k + 1) and HL and TT[k]:
-                product(k + 1, "hn")
 
-        L = NU - 1
-        for j in store_of(NU):
-            store(j)
-        add_bank(L, "in")
-        h_minus_n(L - 1)
-        add_bank(L, "t")
-        candidate(L)
-        times_z(L - 1)
-        for j in range(NU):
-            if GL[j] and j + 3 >= NU:
-                sum_zd(j)
-                faction_term(j)
-        faction_term(L - 1)
-        h_minus_n(L)
+        k = NU - 1
+        for j, f in stores(NU):
+            store(j, f)
+        add_to_aa(k, "in")
+        h_minus_n(k - 1)
+        add_to_aa(k, "t")
+        candidate(k)
+        times_z_and_sum(k - 1)
+        last_faction_term(k - 1)
+        h_minus_n(k)
         for f in range(2):
-            for j in back_of(NU):
+            for j in backs(NU):
                 transpose_back(j, (f,))
-        for j in store_of(NU + 1):
-            store(j, (0,))
-        times_z(L)
-        faction_term(L)
-        for j in back_of(NU + 1):
+        for j, f in stores(NU + 1):
+            if f == 0:
+                store(j, f)
+        times_z_and_sum(k)
+        last_faction_term(k)
+        for j in backs(NU + 1):
             transpose_back(j)
-        for j in store_of(NU + 1):
-            store(j, (1,))
-        for j in back_of(NU + 2):
+        for j, f in stores(NU + 1):
+            if f == 1:
+                store(j, f)
+        for j in backs(NU + 2):
             transpose_back(j)
-        for j in store_of(NU + 2):
-            store(j)
-        for j in store_of(NU + 3):
-            store(j)
+        for j, f in stores(NU + 3):
+            store(j, f)

from contextlib import ExitStack

import concourse.mybir as mybir
from concourse.masks import make_identity

F32 = mybir.dt.float32
BF16 = mybir.dt.bfloat16
U32 = mybir.dt.uint32
U8 = mybir.dt.uint8
FP8X4 = mybir.dt.float8_e4m3fn_x4
ALU = mybir.AluOpType
ACT = mybir.ActivationFunctionType

P = 128
CELLS = 2048
HID = 512
FAC = 256
RANGE = 512
GATES = 3
FLOPS = 2 * 2 * CELLS * HID * GATES * HID
BLEND = 0.85
KAPPA = 0.15 / (BLEND * FAC)

LONG = range(5, 13)
LAST = 2
HEAD = 7
HEAD_ON_VECTOR = (1, 4)
WARM = 4


def tile_phiaslossengine_pb_kernel(tc, ag_diff, tension, hiddens, W_io, w_it, W_hh, b_ih, b_hh, out):
    nc = tc.nc
    with ExitStack() as ctx:
        const = ctx.enter_context(tc.tile_pool(name="const", bufs=1))
        grp = ctx.enter_context(tc.tile_pool(name="grp", bufs=4))
        work = ctx.enter_context(tc.tile_pool(name="work", bufs=6))
        small = ctx.enter_context(tc.tile_pool(name="small", bufs=4))
        outp = ctx.enter_context(tc.tile_pool(name="outp", bufs=6))
        psum = ctx.enter_context(tc.psum_pool(name="psum", bufs=1))
        ctx.enter_context(tc.manual_schedule())

        ident = const.tile([P, P], F32, name="ident")
        identb = const.tile([P, P], BF16, name="identb")
        vrows = const.tile([P, 4, P], F32, name="vrows")
        vec = const.tile([P, 36], F32, name="vec")
        brz = const.tile([P, 8], F32, name="brz")
        table = const.tile([P, 2], F32, name="table")
        zero = const.tile([P, RANGE], BF16, name="zero")
        junk = const.tile([P, RANGE], F32, name="junk")
        trow = const.tile([P, CELLS + HID], BF16, name="trow")
        wrow = const.tile([P, 2, 2, P], BF16, name="wrow")
        tb = const.tile([P, CELLS], BF16, name="tb")
        raw = {
            "a": const.tile([P, CELLS // P, HID], BF16, name="a_raw"),
            "h": const.tile([P, CELLS // P, HID], BF16, name="h_raw"),
            "wio": const.tile([P, 2, 2, GATES, HID], BF16, name="wio_raw"),
            "whh": const.tile([P, 2, 2, GATES, HID], BF16, name="whh_raw"),
        }
        gh = const.tile([P, CELLS // FAC, 2, P, 4], BF16, name="gh", align_bytes=64)
        width = {"a": CELLS, "h": CELLS, "w": 2 * GATES * HID}
        code = {}
        scl = {}
        for nm in ("a", "h", "w"):
            code[nm] = const.tile([P, width[nm]], U32, name="code_" + nm, align_bytes=64)
            scl[nm] = const.tile([P, width[nm]], U8, name="scl_" + nm, align_bytes=64)

        dview = {
            "a": ag_diff.rearrange("(t p) k -> p t k", p=P),
            "h": hiddens.rearrange("(t p) k -> p t k", p=P),
            "wio": W_io.rearrange("(g u p e) k -> p u e g k", u=2, p=P, e=2),
            "whh": W_hh.rearrange("(g u p e) k -> p u e g k", u=2, p=P, e=2),
        }
        oview = out.rearrange("(t p) j -> p t j", p=P)

        units = [(c0, u, e) for u in range(2) for c0 in range(0, CELLS, RANGE) for e in range(2)]
        NU = len(units)

        nc.vector.memset(zero[:], 0.0)
        nc.vector.memset(table[:, 0:1], 0.0)
        nc.vector.memset(vrows[:], 0.0)
        nc.vector.memset(trow[:].bitcast(U32), 0)
        nc.scalar.activation(out=table[:, 1:2], in_=table[:, 0:1], func=ACT.Sigmoid)

        banks = []

        def load_cells(c0):
            t0 = c0 // P
            piece = FAC // P if c0 == 0 else RANGE // P
            for nm in ("a", "h"):
                for t in range(t0, t0 + RANGE // P, piece):
                    nc.sync.dma_start(out=raw[nm][:, t : t + piece, :], in_=dview[nm][:, t : t + piece, :])
                banks.extend([(nm, f) for f in range(c0 // FAC, (c0 + RANGE) // FAC)])

        def load_weights(u, e):
            for nm in ("wio", "whh"):
                nc.sync.dma_start(out=raw[nm][:, u, e, :, :], in_=dview[nm][:, u, e, :, :])
            banks.extend([("w", (u * 2 + e) * GATES + g) for g in range(GATES)])

        load_cells(0)
        for v, src in enumerate((w_it, b_ih, b_hh)):
            nc.sync.dma_start(out=vrows[0:6, v, :].bitcast(BF16), in_=src.rearrange("(b w) -> b w", w=2 * P))
        nc.sync.dma_start(out=vrows[0:8, 3, :].bitcast(BF16), in_=tension.rearrange("(b w) o -> b (w o)", w=2 * P))
        load_weights(0, 0)
        load_weights(0, 1)
        nc.sync.dma_start(out=trow[0:1, 0:CELLS], in_=tension.rearrange("c o -> o c"))
        nc.sync.dma_start(out=trow[0:1, CELLS : CELLS + HID], in_=w_it[2 * HID : 3 * HID].rearrange("(o j) -> o j", o=1))
        for c0 in range(RANGE, CELLS, RANGE):
            load_cells(c0)
        load_weights(1, 0)
        load_weights(1, 1)

        make_identity(nc, ident[:])
        make_identity(nc, identb[:])

        sizes = (3, 4, 4, 4, 2) + (1,) * 4
        waves = []
        first = HEAD
        for size in sizes:
            waves.append(list(range(first, first + size)))
            first += size
        second = set()
        for wave in waves:
            second.update(wave[1::2])

        def wave_of(k):
            return waves[k] if k < len(waves) else []

        def wave_tag(k, i):
            if k < 4:
                return "b%d" % (4 + i % 4)
            return "b%d" % (6 + i % 2) if k == 4 else "b7"

        st = {}

        def bank_transpose(i, tag):
            nm, j = banks[i]
            xt = psum.tile([P, 2, 2, P], F32, tag=tag, name="xt%d" % i)
            for t in range(2):
                if nm == "w":
                    rows = raw[("wio", "whh")[t]][:, j // (2 * GATES), (j // GATES) % 2, j % GATES, :].bitcast(F32)
                else:
                    rows = raw[nm][:, 2 * j + t, :].bitcast(F32)
                for w in range(2):
                    nc.tensor.transpose(xt[:, t, w, :], rows[:, w * P : (w + 1) * P], ident[:])
            st[("xt", i)] = xt

        def bank_copy(i, engine):
            nm, j = banks[i]
            if nm == "h":
                g = gh[:, j]
            elif i in second:
                g = st[("grp", i - 1)][:, 1]
            else:
                st[("grp", i)] = grp.tile([P, 2, 2, P, 4], BF16, tag="grp", name="grp%d" % i, align_bytes=64)
                g = st[("grp", i)][:, 0]
            words = st[("xt", i)][:].rearrange("q t w r -> q t r w")
            if engine == "vector":
                nc.vector.tensor_copy(out=g.bitcast(F32), in_=words)
            else:
                nc.scalar.copy(out=g.bitcast(F32), in_=words)

        def bank_quantise(i):
            if i in second:
                return
            nm, j = banks[i]
            n = 2 if i + 1 in second else 1
            cols = slice(j * FAC, (j + n) * FAC)
            src = gh[:, j : j + n] if nm == "h" else st[("grp", i)][:, 0:n]
            nc.vector.quantize_mx(
                out=code[nm][:, cols].bitcast(FP8X4),
                scales=scl[nm][:, cols],
                in_=src.rearrange("q b t r j -> q (b t r j)"),
            )

        def wave_transpose(k):
            for i in wave_of(k):
                bank_transpose(i, wave_tag(k, i))

        def spread_vectors(tag):
            vps = psum.tile([P, 512], F32, tag=tag, name="vps")
            for v in range(3):
                nc.tensor.transpose(vps[:, v * P : (v + 1) * P], vrows[:, v, :], ident[:])
            for v in range(3):
                nc.vector.tensor_copy(out=vec[:, 12 * v : 12 * v + 12], in_=vps[:, v * P : v * P + 6].bitcast(BF16))
            nc.vector.tensor_tensor(out=brz[:], in0=vec[:, 12:20], in1=vec[:, 24:32], op=ALU.add)

        def spread_tension(half, tag):
            tp = psum.tile([P, 1024], BF16, tag=tag, name="tp%d" % half)
            for f in range(4):
                r = 4 * half + f
                nc.tensor.matmul(
                    out=tp[:, f * FAC : (f + 1) * FAC],
                    lhsT=identb[:, r : r + 1].to_broadcast([P, P]),
                    rhs=vrows[:, 3, :].bitcast(BF16),
                    start=True,
                    stop=True,
                )
            nc.scalar.copy(out=tb[:, half * 1024 : (half + 1) * 1024], in_=tp[:])

        def column(v, g, k):
            c0, u, e = units[k]
            c = ((v * GATES + g) * 2 + u) * 2 + e
            return vec[:, c : c + 1]

        def mx_pass(acc, m, g, k, start, stop):
            c0, u, e = units[k]
            x = ("a", "h")[m]
            o = (((u * 2 + e) * GATES + g) * 2 + m) * P
            nc.tensor.matmul_mx(
                out=acc[:],
                lhsT=code["w"][:, o : o + P].bitcast(FP8X4),
                lhsT_scale=scl["w"][:, o : o + P],
                rhs=code[x][:, c0 : c0 + RANGE].bitcast(FP8X4),
                rhs_scale=scl[x][:, c0 : c0 + RANGE],
                start=start,
                stop=stop,
            )

        def product(k, nm):
            acc = psum.tile([P, RANGE], F32, tag="b%d" % ("r", "z", "in", "hn").index(nm), name="p%s%d" % (nm, k))
            if nm in ("r", "z"):
                g = ("r", "z").index(nm)
                mx_pass(acc, 0, g, k, True, False)
                mx_pass(acc, 1, g, k, False, True)
            else:
                mx_pass(acc, ("in", "hn").index(nm), 2, k, True, True)
            st[(nm, k)] = acc

        def outer_product(k):
            c0, u, e = units[k]
            acc = psum.tile([P, RANGE], F32, tag="b6", name="pt%d" % k)
            nc.tensor.matmul(out=acc[:], lhsT=wrow[:, u, e, :], rhs=trow[:, c0 : c0 + RANGE], start=True, stop=True)
            st[("t", k)] = acc

        def add_tension(k, g, src, dst):
            c0, u, e = units[k]
            t = work.tile([P, RANGE], F32, tag=dst, name="%s%d" % (dst, k))
            nc.vector.scalar_tensor_tensor(
                out=t[:], in0=tb[:, c0 : c0 + RANGE], scalar=column(0, g, k), in1=st[(src, k)][:], op0=ALU.mult, op1=ALU.add
            )
            st[(dst, k)] = t

        def sigmoid(k, g, nm):
            c0, u, e = units[k]
            c = (g * 2 + u) * 2 + e
            t = st[(nm, k)]
            nc.scalar.activation(out=t[:], in_=t[:], func=ACT.Sigmoid, bias=brz[:, c : c + 1], scale=1.0)

        def reset_times_hn(k):
            t = work.tile([P, RANGE], F32, tag="aa", name="aa%d" % k)
            nc.vector.scalar_tensor_tensor(
                out=t[:], in0=st[("hn", k)][:], scalar=column(2, 2, k), in1=st[("rp", k)][:], op0=ALU.add, op1=ALU.mult
            )
            st[("aa", k)] = t

        def add_to_aa(k, nm):
            t = st[("aa", k)]
            nc.vector.tensor_tensor(out=t[:], in0=t[:], in1=st[(nm, k)][:], op=ALU.add)

        def candidate(k):
            t = work.tile([P, RANGE], F32, tag="nn", name="nn%d" % k)
            sn = small.tile([P, 2], F32, tag="sn", name="sn%d" % k)
            for f in range(2):
                cs = slice(f * FAC, (f + 1) * FAC)
                nc.scalar.activation(
                    out=t[:, cs], in_=st[("aa", k)][:, cs], func=ACT.Tanh, bias=column(1, 2, k), scale=1.0,
                    accum_out=sn[:, f : f + 1],
                )
            st[("nn", k)] = t
            st[("sn", k)] = sn

        ghv = gh[:].rearrange("q f t r j -> q (f t r) j")

        def h_minus_n(k):
            c0, u, e = units[k]
            t = work.tile([P, RANGE], F32, tag="dd", name="dd%d" % k)
            engine = nc.gpsimd if k < NU - LAST else nc.vector
            parts = 2 if k == NU - 1 else 1
            for i in range(parts):
                a, b = i * RANGE // parts, (i + 1) * RANGE // parts
                engine.tensor_tensor(
                    out=t[:, a:b], in0=ghv[:, c0 + a : c0 + b, 2 * u + e], in1=st[("nn", k)][:, a:b], op=ALU.subtract
                )
            st[("dd", k)] = t

        def times_z(k):
            t = st[("dd", k)]
            engine = nc.gpsimd if k in LONG else nc.vector
            engine.tensor_tensor(out=t[:], in0=t[:], in1=st[("zp", k)][:], op=ALU.mult)

        def sum_zd(k):
            se = small.tile([P, 2], F32, tag="se", name="se%d" % k)
            for f in range(2):
                cs = slice(f * FAC, (f + 1) * FAC)
                nc.scalar.activation(
                    out=junk[:, cs], in_=st[("dd", k)][:, cs], func=ACT.Identity, bias=0.0, scale=KAPPA,
                    accum_out=se[:, f : f + 1],
                )
            st[("se", k)] = se

        def faction_term(k):
            fm = small.tile([P, 2], F32, tag="fm", name="fm%d" % k)
            for f in range(2):
                nc.scalar.activation(
                    out=fm[:, f : f + 1], in_=st[("sn", k)][:, f : f + 1], func=ACT.Identity, scale=KAPPA,
                    bias=st[("se", k)][:, f : f + 1],
                )
            st[("fm", k)] = fm

        def times_z_and_sum(k):
            t = st[("dd", k)]
            se = small.tile([P, 2], F32, tag="se", name="se%d" % k)
            for f in range(2):
                cs = slice(f * FAC, (f + 1) * FAC)
                nc.vector.scalar_tensor_tensor(
                    out=t[:, cs], in0=t[:, cs], scalar=1.0, in1=st[("zp", k)][:, cs], op0=ALU.mult, op1=ALU.mult,
                    accum_out=se[:, f : f + 1],
                )
            st[("se", k)] = se

        def last_faction_term(k):
            sk = small.tile([P, 2], F32, tag="sk", name="sk%d" % k)
            fm = small.tile([P, 2], F32, tag="fm", name="fm%d" % k)
            nc.scalar.mul(out=sk[:], in_=st[("sn", k)][:], mul=KAPPA)
            for f in range(2):
                nc.scalar.activation(
                    out=fm[:, f : f + 1], in_=st[("se", k)][:, f : f + 1], func=ACT.Identity, scale=KAPPA,
                    bias=sk[:, f : f + 1],
                )
            st[("fm", k)] = fm

        def result_banks(k, f):
            c0, u, e = units[k]
            if k == NU - 2 and f == 1:
                return [psum.tile([P, 1, 2, P], F32, tag="b%d" % t, name="fin%d_%d_%d" % (k, f, t)) for t in range(2)]
            tag = 4 + f if u == 0 else (4, 5, 7)[(c0 // FAC + f) % 3]
            return [psum.tile([P, 2, 2, P], F32, tag="b%d" % tag, name="fin%d_%d" % (k, f))]

        def transpose_back(k, factions=(0, 1)):
            c0, u, e = units[k]
            for f in factions:
                if e == 0:
                    st[("fin", c0, u, f)] = result_banks(k, f)
                fin = st[("fin", c0, u, f)]
                for t in range(2):
                    block = fin[t][:, 0, e, :] if len(fin) == 2 else fin[0][:, t, e, :]
                    cs = slice((2 * f + t) * P, (2 * f + t + 1) * P)
                    terms = (st[("nn", k)][:, cs], st[("dd", k)][:, cs], st[("fm", k)][:, f : f + 1].to_broadcast([P, P]))
                    for x, term in enumerate(terms):
                        nc.tensor.matmul(
                            out=block, lhsT=term, rhs=ident[:], is_transpose=True, start=(x == 0), stop=(x == 2)
                        )

        def copy_scaled(engine, o, fin):
            src = fin[:].rearrange("c t e p -> c t p e")
            if engine == "vector":
                nc.vector.tensor_scalar(out=o, in0=src, scalar1=BLEND, scalar2=0.0, op0=ALU.mult, op1=ALU.add)
            else:
                nc.scalar.mul(out=o, in_=src, mul=BLEND)

        def store(k, f):
            c0, u, e = units[k]
            fin = st[("fin", c0, u, f)]
            n = 2 // len(fin)
            o = outp.tile([P, 2, P, 2], F32, tag="osb", name="osb%d_%d" % (k, f))
            for i, bank in enumerate(fin):
                on_vector = k >= LONG.stop and f == 1 and i == 0
                t = i * n
                copy_scaled("vector" if on_vector else "scalar", o[:, t : t + n], bank)
                t0 = c0 // P + 2 * f + t
                nc.sync.dma_start(
                    out=oview[:, t0 : t0 + n, u * FAC : (u + 1) * FAC], in_=o[:, t : t + n].rearrange("c t p e -> c t (p e)")
                )

        for x in range(WARM):
            acc = psum.tile([P, RANGE], F32, tag="b3", name="zz%d" % x)
            nc.tensor.matmul(out=acc[:], lhsT=zero[:, 0:P], rhs=zero[:], start=True, stop=True)
        for i in range(HEAD):
            if i == HEAD - GATES:
                spread_vectors("b0")
                spread_tension(0, "b1")
                spread_tension(1, "b0")
            bank_transpose(i, "b%d" % (2 + i % 6))
            bank_copy(i, "vector" if i in HEAD_ON_VECTOR else "scalar")
            if i >= 1:
                bank_quantise(i - 1)
        for i in wave_of(0):
            bank_transpose(i, wave_tag(0, i))
            bank_copy(i, "scalar")
        bank_quantise(HEAD - 1)
        for nm in ("r", "z", "hn", "in"):
            product(0, nm)
        wave_transpose(1)

        def back_period(k):
            return k + (4 if k in LONG else 3)

        def backs(period):
            return [k for k in range(NU) if back_period(k) == period]

        store_period = {}
        for k in range(1, NU, 2):
            done = back_period(k) + 1
            store_period[(k, 0)] = done
            store_period[(k, 1)] = done + 1 if units[k][1] == 1 and done + 1 < NU else done

        def stores(period):
            return [key for key in store_period if store_period[key] == period]

        for k in range(NU):
            if k - 2 in LONG:
                h_minus_n(k - 2)
                times_z(k - 2)
            add_tension(k, 0, "r", "rp")
            sigmoid(k, 0, "rp")
            if k - 1 >= LONG.start:
                add_to_aa(k - 1, "in")
            add_tension(k, 1, "z", "zp")
            if k - 3 in LONG:
                sum_zd(k - 3)
            sigmoid(k, 1, "zp")
            if k - 1 >= LONG.start:
                add_to_aa(k - 1, "t")
            if k < LONG.start:
                add_tension(k, 2, "in", "cc")
                for i in wave_of(k):
                    bank_quantise(i)
            if 0 <= k - 1 < LONG.start:
                add_to_aa(k - 1, "cc")
            if k >= 1:
                candidate(k - 1)
            if 0 <= k - 3 < LONG.stop:
                faction_term(k - 3)
            for j, f in stores(k):
                store(j, f)
            for i in wave_of(k + 1):
                bank_copy(i, "scalar")
            if k == LONG.start - 2:
                w_n = trow[:, CELLS : CELLS + HID].rearrange("p (u m e) -> p u e m", u=2, e=2)
                nc.scalar.copy(out=wrow[:], in_=w_n)
            reset_times_hn(k)
            if k >= LONG.start:
                for i in wave_of(k):
                    bank_quantise(i)
            if 0 <= k - 2 < LONG.start:
                times_z(k - 2)
                sum_zd(k - 2)
            if k - 2 >= LONG.stop:
                times_z_and_sum(k - 2)
            if 0 <= k - 1 < LONG.start or LONG.stop <= k - 1 < NU - LAST:
                h_minus_n(k - 1)
            if k - 2 >= LONG.stop:
                last_faction_term(k - 2)
            if k + 1 < NU:
                product(k + 1, "r")
            if k >= LONG.start:
                product(k, "in")
            if k + 1 < NU:
                product(k + 1, "z")
                product(k + 1, "hn")
            if k + 1 < LONG.start:
                product(k + 1, "in")
            if k >= LONG.start:
                outer_product(k)
            for j in backs(k):
                transpose_back(j)
            wave_transpose(k + 2)

        k = NU - 1
        for j, f in stores(NU):
            store(j, f)
        add_to_aa(k, "in")
        h_minus_n(k - 1)
        add_to_aa(k, "t")
        candidate(k)
        times_z_and_sum(k - 1)
        last_faction_term(k - 1)
        h_minus_n(k)
        for f in range(2):
            for j in backs(NU):
                transpose_back(j, (f,))
        for j, f in stores(NU + 1):
            if f == 0:
                store(j, f)
        times_z_and_sum(k)
        last_faction_term(k)
        for j in backs(NU + 1):
            transpose_back(j)
        for j, f in stores(NU + 1):
            if f == 1:
                store(j, f)
        for j in backs(NU + 2):
            transpose_back(j)
        for j, f in stores(NU + 3):
            store(j, f)
